import numpy as np
import ml_dtypes


def mxq(x, axis, fmt="e4m3"):
    dtype, down = {"e4m3": (ml_dtypes.float8_e4m3fn, 7), "e5m2": (ml_dtypes.float8_e5m2, 14)}[fmt]
    v = np.moveaxis(np.asarray(x, np.float32).astype(ml_dtypes.bfloat16).astype(np.float64), axis, -1)
    blocks = v.reshape(v.shape[:-1] + (-1, 32))
    amax = np.abs(blocks).max(-1, keepdims=True)
    byte = np.maximum(np.where(amax > 0, np.frexp(amax)[1] - 1 + 127, 0) - down, 1)
    scale = np.exp2(byte - 127.0)
    codes = (blocks / scale).astype(np.float32).astype(dtype).astype(np.float64)
    return np.moveaxis((codes * scale).reshape(v.shape), -1, axis)


WIDE = False


def mx_kscale(k, group=512):
    if not WIDE:
        return np.ones(k)
    levels = np.array([20, -20, 10, -10, 0])
    if group != 512:
        return np.exp2(np.random.permutation(np.resize(levels, k // group))).repeat(group)
    a = np.random.permutation(np.resize(levels, k // 512 * 4)).reshape(k // 512, 4)
    idx = np.arange(k)
    return np.exp2(a[idx // 512, idx % 128 // 32])


BF16 = ml_dtypes.bfloat16


def bf(x):
    return np.asarray(x, np.float32).astype(BF16)


def f64(x):
    return np.asarray(x).astype(np.float64)


B, T, C, CO, HS, DW, DA, DV, DG = 4, 128, 2048, 2048, 64, 128, 128, 128, 256


def sigmoid(u):
    return 1.0 / (1.0 + np.exp(-u))


def setup_inputs():
    n = np.random.standard_normal
    s = mx_kscale(B * T, group=T).reshape(B, T)[:, :1, None]
    x0 = bf(n((B, T, C)))
    x_v = bf(n((1, 1, C)) * 0.3)
    W_v = bf(n((CO, C)) / np.sqrt(C))
    v_hid = bf(n((B, T, DV)))
    v2 = bf(n((DV, CO)) / np.sqrt(DV))
    v0 = bf(0.73 + n((1, 1, CO)) * 0.2)
    v_first = bf(n((B, T, CO)))
    g = bf(n((B, T, CO)) * np.exp2(np.random.randint(-12, 1, (B, T, 1))) / s)
    mix = sigmoid(f64(v0) + f64(v_hid) @ f64(v2))
    return {
        "x": bf(f64(x0) * s),
        "x_v": x_v,
        "W_v": W_v,
        "v_hid": v_hid,
        "v2": v2,
        "v0": v0,
        "v_first": v_first,
        "mix": np.asarray(mix, np.float32),
        "grad_out": g,
    }


def reference(x, x_v, W_v, v_hid, v2, v0, v_first, mix, grad_out):
    x = f64(x)
    prev = np.concatenate([np.zeros_like(x[:, :1]), x[:, :-1]], axis=1)
    xv = (x + (prev - x) * f64(x_v)).reshape(B * T, C)
    dv = (f64(grad_out) * (1.0 - f64(mix))).reshape(B * T, CO)
    return mxq(dv, 0, "e5m2").T @ mxq(xv, 0, "e4m3")

@@ -1,0 +1,192 @@
+from contextlib import ExitStack
+
+import concourse.mybir as mybir
+from concourse.masks import make_identity
+
+F32 = mybir.dt.float32
+BF16 = mybir.dt.bfloat16
+U32 = mybir.dt.uint32
+U8 = mybir.dt.uint8
+E4M3_X4 = mybir.dt.float8_e4m3fn_x4
+E5M2_X4 = mybir.dt.float8_e5m2_x4
+ALU = mybir.AluOpType
+
+P = 128
+PACK = 4
+TOKENS = P * PACK
+SEQ_PARTITIONS = 128 // PACK
+C = 2048
+CO = 2048
+N_TILE = 512
+M_TILE = 128
+N_CHUNKS = C // N_TILE
+M_TILES = CO // M_TILE
+M_TILES_PER_CHUNK = N_TILE // M_TILE
+
+FLOPS = 2 * TOKENS * CO * C
+BYTES = 2 * TOKENS * C + 2 * C + 4 * TOKENS * CO + 2 * TOKENS * CO + 4 * CO * C
+
+
+def tile_full_tmix_params_pb_v_kernel(
+    tc, x, x_v, W_v, v_hid, v2, v0, v_first, mix, grad_out, out
+):
+    nc = tc.nc
+    x_rows = x.rearrange("b (q j) c -> (b q) j c", j=PACK)
+    mix_rows = mix.rearrange("b (q j) c -> (b q) j c", j=PACK)
+    grad_rows = grad_out.rearrange("b (q j) c -> (b q) j c", j=PACK)
+
+    with ExitStack() as ctx:
+        consts = ctx.enter_context(tc.tile_pool(name="consts", bufs=1))
+        inputs = ctx.enter_context(tc.tile_pool(name="inputs", bufs=1))
+        keep = ctx.enter_context(tc.tile_pool(name="keep", bufs=1))
+        work = ctx.enter_context(tc.tile_pool(name="work", bufs=2))
+        stage_pool = ctx.enter_context(tc.tile_pool(name="stage", bufs=6))
+        banks = ctx.enter_context(tc.psum_pool(name="banks", bufs=6))
+        prev_banks = ctx.enter_context(tc.psum_pool(name="prev_banks", bufs=2))
+
+        x_v_row0 = consts.tile([P, C], BF16)
+        nc.vector.memset(x_v_row0[:], 0.0)
+        nc.sync.dma_start(out=x_v_row0[0:1, :], in_=x_v.rearrange("a b c -> (a b) c"))
+
+        x_chunks = []
+        for n in range(N_CHUNKS):
+            x_chunks.append(inputs.tile([P, PACK, N_TILE], BF16, name="x_chunk%d" % n))
+
+        def load_x_chunk(n):
+            nc.sync.dma_start(
+                out=x_chunks[n][:], in_=x_rows[:, :, n * N_TILE : (n + 1) * N_TILE]
+            )
+
+        mix_sb = inputs.tile([P, PACK, CO], F32)
+        grad_sb = inputs.tile([P, PACK, CO], BF16)
+        load_x_chunk(0)
+        load_x_chunk(1)
+        nc.sync.dma_start(out=mix_sb[:, 0:2, :], in_=mix_rows[:, 0:2, :])
+        nc.sync.dma_start(out=mix_sb[:, 2:4, :], in_=mix_rows[:, 2:4, :])
+        nc.sync.dma_start(out=grad_sb[:], in_=grad_rows)
+        load_x_chunk(2)
+        load_x_chunk(3)
+
+        ones = consts.tile([P, P], BF16)
+        nc.gpsimd.memset(ones[:], 1.0)
+        shift_wide = consts.tile([P, P + 1], BF16)
+        make_identity(nc, shift_wide[:, 1 : P + 1])
+        shift = shift_wide[:, 0:P]
+        nc.gpsimd.memset(
+            shift.rearrange("k (s m) -> k s m", m=SEQ_PARTITIONS)[:, :, 0:1], 0.0
+        )
+
+        x_v_all = consts.tile([P, C], BF16)
+        for n in range(N_CHUNKS):
+            cols = slice(n * N_TILE, (n + 1) * N_TILE)
+            spread = banks.tile([P, N_TILE], F32, tag="bank")
+            nc.tensor.matmul(
+                out=spread[:], lhsT=ones[:], rhs=x_v_row0[:, cols], start=True, stop=True
+            )
+            nc.scalar.copy(out=x_v_all[:, cols], in_=spread[:])
+
+        xv_codes = keep.tile([P, C], U32, align_bytes=64)
+        xv_scales = keep.tile([P, C], U8, align_bytes=64)
+        dv_codes = keep.tile([P, CO], U32, align_bytes=64)
+        dv_scales = keep.tile([P, CO], U8, align_bytes=64)
+
+        def shift_row3(n):
+            prev_row0 = prev_banks.tile([P, N_TILE], F32, tag="prev_row0")
+            nc.tensor.matmul(
+                out=prev_row0[:],
+                lhsT=shift,
+                rhs=x_chunks[n][:, PACK - 1, :],
+                start=True,
+                stop=True,
+            )
+            return prev_row0
+
+        def quantise_xv(n, prev_row0):
+            cols = slice(n * N_TILE, (n + 1) * N_TILE)
+            x_n = x_chunks[n]
+            term = work.tile([P, PACK, N_TILE], F32)
+            nc.vector.tensor_tensor(
+                out=term[:, 1:PACK, :],
+                in0=x_n[:, 1:PACK, :],
+                in1=x_n[:, 0 : PACK - 1, :],
+                op=ALU.subtract,
+            )
+            nc.vector.tensor_tensor(
+                out=term[:, 0, :], in0=x_n[:, 0, :], in1=prev_row0[:], op=ALU.subtract
+            )
+            nc.vector.tensor_tensor(
+                out=term[:],
+                in0=term[:],
+                in1=x_v_all[:, cols].unsqueeze(1).to_broadcast([P, PACK, N_TILE]),
+                op=ALU.mult,
+            )
+            xv_grouped = work.tile([P, N_TILE, PACK], BF16, align_bytes=64)
+            nc.vector.tensor_tensor(
+                out=xv_grouped[:],
+                in0=term[:].rearrange("p j w -> p w j"),
+                in1=x_n[:].rearrange("p j w -> p w j"),
+                op=ALU.subtract,
+            )
+            nc.vector.quantize_mx(
+                out=xv_codes[:, cols].bitcast(E4M3_X4),
+                scales=xv_scales[:, cols],
+                in_=xv_grouped[:].rearrange("p w j -> p (w j)"),
+            )
+
+        def quantise_dv(d):
+            cols = slice(d * N_TILE, (d + 1) * N_TILE)
+            dv_grouped = work.tile([P, N_TILE, PACK], BF16, align_bytes=64)
+            nc.vector.scalar_tensor_tensor(
+                out=dv_grouped[:],
+                in0=mix_sb[:, :, cols].rearrange("p j w -> p w j"),
+                scalar=1.0,
+                in1=grad_sb[:, :, cols].rearrange("p j w -> p w j"),
+                op0=ALU.subtract,
+                op1=ALU.mult,
+            )
+            nc.vector.quantize_mx(
+                out=dv_codes[:, cols].bitcast(E5M2_X4),
+                scales=dv_scales[:, cols],
+                in_=dv_grouped[:].rearrange("p w j -> p (w j)"),
+            )
+
+        def multiply_and_store(m, first_chunk, chunks, vector_helps):
+            rows = slice(m * M_TILE, (m + 1) * M_TILE)
+            stage = stage_pool.tile([P, chunks * N_TILE], F32, tag="stage%d" % chunks)
+            for i in range(chunks):
+                cols = slice((first_chunk + i) * N_TILE, (first_chunk + i + 1) * N_TILE)
+                product = banks.tile([P, N_TILE], F32, tag="bank")
+                nc.tensor.matmul_mx(
+                    out=product[:],
+                    lhsT=dv_codes[:, rows].bitcast(E5M2_X4),
+                    lhsT_scale=dv_scales[:, rows],
+                    rhs=xv_codes[:, cols].bitcast(E4M3_X4),
+                    rhs_scale=xv_scales[:, cols],
+                    start=True,
+                    stop=True,
+                )
+                stage_cols = stage[:, i * N_TILE : (i + 1) * N_TILE]
+                if vector_helps and m % 2 == 1:
+                    nc.vector.tensor_copy(out=stage_cols, in_=product[:])
+                else:
+                    nc.scalar.copy(out=stage_cols, in_=product[:])
+            nc.sync.dma_start(
+                out=out[rows, first_chunk * N_TILE : (first_chunk + chunks) * N_TILE],
+                in_=stage[:],
+            )
+
+        prev_rows = [shift_row3(0), shift_row3(1)]
+        quantise_xv(0, prev_rows[0])
+        quantise_xv(1, prev_rows[1])
+        prev_rows.append(shift_row3(2))
+        prev_rows.append(shift_row3(3))
+        for d in range(N_CHUNKS):
+            quantise_dv(d)
+            for m in range(d * M_TILES_PER_CHUNK, (d + 1) * M_TILES_PER_CHUNK):
+                multiply_and_store(m, 0, 2, False)
+        quantise_xv(2, prev_rows[2])
+        for m in range(M_TILES):
+            multiply_and_store(m, 2, 1, False)
+        quantise_xv(3, prev_rows[3])
+        for m in range(M_TILES):
+            multiply_and_store(m, 3, 1, True)

@@ -17,11 +17,15 @@ TOKENS = P * PACK
 SEQ_PARTITIONS = 128 // PACK
 C = 2048
 CO = 2048
-N_TILE = 512
+CHUNK = 512
+PIECE = CHUNK // 2
+PIECES = CHUNK // PIECE
 M_TILE = 128
-N_CHUNKS = C // N_TILE
+X_CHUNKS = C // CHUNK
+DV_CHUNKS = CO // CHUNK
 M_TILES = CO // M_TILE
-M_TILES_PER_CHUNK = N_TILE // M_TILE
+M_TILES_PER_CHUNK = CHUNK // M_TILE
+LOAD_COLS = 2 * CHUNK
 
 FLOPS = 2 * TOKENS * CO * C
 BYTES = 2 * TOKENS * C + 2 * C + 4 * TOKENS * CO + 2 * TOKENS * CO + 4 * CO * C
@@ -36,6 +40,7 @@ def tile_full_tmix_params_pb_v_kernel(
     grad_rows = grad_out.rearrange("b (q j) c -> (b q) j c", j=PACK)
 
     with ExitStack() as ctx:
+        ctx.enter_context(tc.manual_schedule())
         consts = ctx.enter_context(tc.tile_pool(name="consts", bufs=1))
         inputs = ctx.enter_context(tc.tile_pool(name="inputs", bufs=1))
         keep = ctx.enter_context(tc.tile_pool(name="keep", bufs=1))
@@ -49,21 +54,26 @@ def tile_full_tmix_params_pb_v_kernel(
         nc.sync.dma_start(out=x_v_row0[0:1, :], in_=x_v.rearrange("a b c -> (a b) c"))
 
         x_chunks = []
-        for n in range(N_CHUNKS):
-            x_chunks.append(inputs.tile([P, PACK, N_TILE], BF16, name="x_chunk%d" % n))
+        for n in range(X_CHUNKS):
+            x_chunks.append(inputs.tile([P, PACK, CHUNK], BF16, name="x_chunk%d" % n))
+        mix_loads = []
+        grad_loads = []
+        for i in range(CO // LOAD_COLS):
+            mix_loads.append(inputs.tile([P, PACK, LOAD_COLS], F32, name="mix_load%d" % i))
+            grad_loads.append(inputs.tile([P, PACK, LOAD_COLS], BF16, name="grad_load%d" % i))
 
         def load_x_chunk(n):
-            nc.sync.dma_start(
-                out=x_chunks[n][:], in_=x_rows[:, :, n * N_TILE : (n + 1) * N_TILE]
-            )
+            nc.sync.dma_start(out=x_chunks[n][:], in_=x_rows[:, :, n * CHUNK : (n + 1) * CHUNK])
 
-        mix_sb = inputs.tile([P, PACK, CO], F32)
-        grad_sb = inputs.tile([P, PACK, CO], BF16)
+        def load_mix_and_grad(i):
+            cols = slice(i * LOAD_COLS, (i + 1) * LOAD_COLS)
+            nc.sync.dma_start(out=grad_loads[i][:], in_=grad_rows[:, :, cols])
+            nc.sync.dma_start(out=mix_loads[i][:], in_=mix_rows[:, :, cols])
+
         load_x_chunk(0)
+        load_mix_and_grad(0)
         load_x_chunk(1)
-        nc.sync.dma_start(out=mix_sb[:, 0:2, :], in_=mix_rows[:, 0:2, :])
-        nc.sync.dma_start(out=mix_sb[:, 2:4, :], in_=mix_rows[:, 2:4, :])
-        nc.sync.dma_start(out=grad_sb[:], in_=grad_rows)
+        load_mix_and_grad(1)
         load_x_chunk(2)
         load_x_chunk(3)
 
@@ -72,14 +82,12 @@ def tile_full_tmix_params_pb_v_kernel(
         shift_wide = consts.tile([P, P + 1], BF16)
         make_identity(nc, shift_wide[:, 1 : P + 1])
         shift = shift_wide[:, 0:P]
-        nc.gpsimd.memset(
-            shift.rearrange("k (s m) -> k s m", m=SEQ_PARTITIONS)[:, :, 0:1], 0.0
-        )
+        nc.gpsimd.memset(shift.rearrange("k (s m) -> k s m", m=SEQ_PARTITIONS)[:, :, 0:1], 0.0)
 
         x_v_all = consts.tile([P, C], BF16)
-        for n in range(N_CHUNKS):
-            cols = slice(n * N_TILE, (n + 1) * N_TILE)
-            spread = banks.tile([P, N_TILE], F32, tag="bank")
+        for n in range(X_CHUNKS):
+            cols = slice(n * CHUNK, (n + 1) * CHUNK)
+            spread = banks.tile([P, CHUNK], F32, tag="bank")
             nc.tensor.matmul(
                 out=spread[:], lhsT=ones[:], rhs=x_v_row0[:, cols], start=True, stop=True
             )
@@ -91,7 +99,7 @@ def tile_full_tmix_params_pb_v_kernel(
         dv_scales = keep.tile([P, CO], U8, align_bytes=64)
 
         def shift_row3(n):
-            prev_row0 = prev_banks.tile([P, N_TILE], F32, tag="prev_row0")
+            prev_row0 = prev_banks.tile([P, CHUNK], F32, tag="prev_row0")
             nc.tensor.matmul(
                 out=prev_row0[:],
                 lhsT=shift,
@@ -101,61 +109,83 @@ def tile_full_tmix_params_pb_v_kernel(
             )
             return prev_row0
 
-        def quantise_xv(n, prev_row0):
-            cols = slice(n * N_TILE, (n + 1) * N_TILE)
+        def prepare_xv(n, prev_row0):
             x_n = x_chunks[n]
-            term = work.tile([P, PACK, N_TILE], F32)
-            nc.vector.tensor_tensor(
-                out=term[:, 1:PACK, :],
-                in0=x_n[:, 1:PACK, :],
-                in1=x_n[:, 0 : PACK - 1, :],
-                op=ALU.subtract,
-            )
-            nc.vector.tensor_tensor(
-                out=term[:, 0, :], in0=x_n[:, 0, :], in1=prev_row0[:], op=ALU.subtract
-            )
-            nc.vector.tensor_tensor(
-                out=term[:],
-                in0=term[:],
-                in1=x_v_all[:, cols].unsqueeze(1).to_broadcast([P, PACK, N_TILE]),
-                op=ALU.mult,
-            )
-            xv_grouped = work.tile([P, N_TILE, PACK], BF16, align_bytes=64)
-            nc.vector.tensor_tensor(
-                out=xv_grouped[:],
-                in0=term[:].rearrange("p j w -> p w j"),
-                in1=x_n[:].rearrange("p j w -> p w j"),
-                op=ALU.subtract,
-            )
-            nc.vector.quantize_mx(
-                out=xv_codes[:, cols].bitcast(E4M3_X4),
-                scales=xv_scales[:, cols],
-                in_=xv_grouped[:].rearrange("p w j -> p (w j)"),
-            )
+            piece_cols = [slice(h * PIECE, (h + 1) * PIECE) for h in range(PIECES)]
+            terms = []
+            grouped = []
+            for h in range(PIECES):
+                terms.append(work.tile([P, PACK, PIECE], F32, name="term%d" % h))
+                grouped.append(
+                    work.tile([P, PIECE, PACK], BF16, name="xv_grouped%d" % h, align_bytes=64)
+                )
+            for h in range(PIECES):
+                w = piece_cols[h]
+                nc.vector.tensor_tensor(
+                    out=terms[h][:, 1:PACK, :],
+                    in0=x_n[:, 1:PACK, w],
+                    in1=x_n[:, 0 : PACK - 1, w],
+                    op=ALU.subtract,
+                )
+                nc.vector.tensor_tensor(
+                    out=terms[h][:, 0, :], in0=x_n[:, 0, w], in1=prev_row0[:, w], op=ALU.subtract
+                )
+            for h in range(PIECES):
+                first = n * CHUNK + h * PIECE
+                nc.vector.tensor_tensor(
+                    out=terms[h][:],
+                    in0=terms[h][:],
+                    in1=x_v_all[:, first : first + PIECE]
+                    .unsqueeze(1)
+                    .to_broadcast([P, PACK, PIECE]),
+                    op=ALU.mult,
+                )
+            for h in range(PIECES):
+                nc.vector.tensor_tensor(
+                    out=grouped[h][:],
+                    in0=terms[h][:].rearrange("p j w -> p w j"),
+                    in1=x_n[:, :, piece_cols[h]].rearrange("p j w -> p w j"),
+                    op=ALU.subtract,
+                )
+            for h in range(PIECES):
+                cols = slice(n * CHUNK + h * PIECE, n * CHUNK + (h + 1) * PIECE)
+                nc.vector.quantize_mx(
+                    out=xv_codes[:, cols].bitcast(E4M3_X4),
+                    scales=xv_scales[:, cols],
+                    in_=grouped[h][:].rearrange("p w j -> p (w j)"),
+                )
 
-        def quantise_dv(d):
-            cols = slice(d * N_TILE, (d + 1) * N_TILE)
-            dv_grouped = work.tile([P, N_TILE, PACK], BF16, align_bytes=64)
-            nc.vector.scalar_tensor_tensor(
-                out=dv_grouped[:],
-                in0=mix_sb[:, :, cols].rearrange("p j w -> p w j"),
-                scalar=1.0,
-                in1=grad_sb[:, :, cols].rearrange("p j w -> p w j"),
-                op0=ALU.subtract,
-                op1=ALU.mult,
-            )
-            nc.vector.quantize_mx(
-                out=dv_codes[:, cols].bitcast(E5M2_X4),
-                scales=dv_scales[:, cols],
-                in_=dv_grouped[:].rearrange("p w j -> p (w j)"),
-            )
+        def prepare_dv(d):
+            mix_sb = mix_loads[d * CHUNK // LOAD_COLS]
+            grad_sb = grad_loads[d * CHUNK // LOAD_COLS]
+            grouped = []
+            for h in range(PIECES):
+                first = d * CHUNK % LOAD_COLS + h * PIECE
+                grouped.append(
+                    work.tile([P, PIECE, PACK], BF16, name="dv_grouped%d" % h, align_bytes=64)
+                )
+                nc.vector.scalar_tensor_tensor(
+                    out=grouped[h][:],
+                    in0=mix_sb[:, :, first : first + PIECE].rearrange("p j w -> p w j"),
+                    scalar=1.0,
+                    in1=grad_sb[:, :, first : first + PIECE].rearrange("p j w -> p w j"),
+                    op0=ALU.subtract,
+                    op1=ALU.mult,
+                )
+            for h in range(PIECES):
+                cols = slice(d * CHUNK + h * PIECE, d * CHUNK + (h + 1) * PIECE)
+                nc.vector.quantize_mx(
+                    out=dv_codes[:, cols].bitcast(E5M2_X4),
+                    scales=dv_scales[:, cols],
+                    in_=grouped[h][:].rearrange("p w j -> p (w j)"),
+                )
 
         def multiply_and_store(m, first_chunk, chunks, vector_helps):
             rows = slice(m * M_TILE, (m + 1) * M_TILE)
-            stage = stage_pool.tile([P, chunks * N_TILE], F32, tag="stage%d" % chunks)
+            stage = stage_pool.tile([P, chunks * CHUNK], F32, tag="stage%d" % chunks)
             for i in range(chunks):
-                cols = slice((first_chunk + i) * N_TILE, (first_chunk + i + 1) * N_TILE)
-                product = banks.tile([P, N_TILE], F32, tag="bank")
+                cols = slice((first_chunk + i) * CHUNK, (first_chunk + i + 1) * CHUNK)
+                product = banks.tile([P, CHUNK], F32, tag="bank")
                 nc.tensor.matmul_mx(
                     out=product[:],
                     lhsT=dv_codes[:, rows].bitcast(E5M2_X4),
@@ -165,28 +195,39 @@ def tile_full_tmix_params_pb_v_kernel(
                     start=True,
                     stop=True,
                 )
-                stage_cols = stage[:, i * N_TILE : (i + 1) * N_TILE]
+                stage_cols = stage[:, i * CHUNK : (i + 1) * CHUNK]
                 if vector_helps and m % 2 == 1:
                     nc.vector.tensor_copy(out=stage_cols, in_=product[:])
                 else:
                     nc.scalar.copy(out=stage_cols, in_=product[:])
             nc.sync.dma_start(
-                out=out[rows, first_chunk * N_TILE : (first_chunk + chunks) * N_TILE],
-                in_=stage[:],
+                out=out[rows, first_chunk * CHUNK : (first_chunk + chunks) * CHUNK], in_=stage[:]
             )
 
-        prev_rows = [shift_row3(0), shift_row3(1)]
-        quantise_xv(0, prev_rows[0])
-        quantise_xv(1, prev_rows[1])
-        prev_rows.append(shift_row3(2))
-        prev_rows.append(shift_row3(3))
-        for d in range(N_CHUNKS):
-            quantise_dv(d)
-            for m in range(d * M_TILES_PER_CHUNK, (d + 1) * M_TILES_PER_CHUNK):
+        def m_tiles_of(d):
+            return range(d * M_TILES_PER_CHUNK, (d + 1) * M_TILES_PER_CHUNK)
+
+        prev_row0 = shift_row3(0)
+        prepare_xv(0, prev_row0)
+        prev_row0 = shift_row3(1)
+        prepare_dv(0)
+        for m in m_tiles_of(0):
+            multiply_and_store(m, 0, 1, False)
+        prepare_xv(1, prev_row0)
+        for m in m_tiles_of(0):
+            multiply_and_store(m, 1, 1, False)
+        prepare_dv(1)
+        for m in m_tiles_of(1):
+            multiply_and_store(m, 0, 2, False)
+        prev_row0_of_2 = shift_row3(2)
+        prev_row0_of_3 = shift_row3(3)
+        for d in range(2, DV_CHUNKS):
+            prepare_dv(d)
+            for m in m_tiles_of(d):
                 multiply_and_store(m, 0, 2, False)
-        quantise_xv(2, prev_rows[2])
+        prepare_xv(2, prev_row0_of_2)
         for m in range(M_TILES):
             multiply_and_store(m, 2, 1, False)
-        quantise_xv(3, prev_rows[3])
+        prepare_xv(3, prev_row0_of_3)
         for m in range(M_TILES):
             multiply_and_store(m, 3, 1, True)

@@ -20,6 +20,7 @@ CO = 2048
 CHUNK = 512
 PIECE = CHUNK // 2
 PIECES = CHUNK // PIECE
+RUN = 4
 M_TILE = 128
 X_CHUNKS = C // CHUNK
 DV_CHUNKS = CO // CHUNK
@@ -51,7 +52,7 @@ def tile_full_tmix_params_pb_v_kernel(
 
         x_v_row0 = consts.tile([P, C], BF16)
         nc.vector.memset(x_v_row0[:], 0.0)
-        nc.sync.dma_start(out=x_v_row0[0:1, :], in_=x_v.rearrange("a b c -> (a b) c"))
+        nc.scalar.dma_start(out=x_v_row0[0:1, :], in_=x_v.rearrange("a b c -> (a b) c"))
 
         x_chunks = []
         for n in range(X_CHUNKS):
@@ -142,9 +143,9 @@ def tile_full_tmix_params_pb_v_kernel(
                 )
             for h in range(PIECES):
                 nc.vector.tensor_tensor(
-                    out=grouped[h][:],
-                    in0=terms[h][:].rearrange("p j w -> p w j"),
-                    in1=x_n[:, :, piece_cols[h]].rearrange("p j w -> p w j"),
+                    out=grouped[h][:].rearrange("p (r i) j -> p r j i", i=RUN),
+                    in0=terms[h][:].rearrange("p j (r i) -> p r j i", i=RUN),
+                    in1=x_n[:, :, piece_cols[h]].rearrange("p j (r i) -> p r j i", i=RUN),
                     op=ALU.subtract,
                 )
             for h in range(PIECES):

@@ -20,7 +20,7 @@ CO = 2048
 CHUNK = 512
 PIECE = CHUNK // 2
 PIECES = CHUNK // PIECE
-RUN = 4
+TENSOR_ROWS = 2
 M_TILE = 128
 X_CHUNKS = C // CHUNK
 DV_CHUNKS = CO // CHUNK
@@ -48,11 +48,10 @@ def tile_full_tmix_params_pb_v_kernel(
         work = ctx.enter_context(tc.tile_pool(name="work", bufs=2))
         stage_pool = ctx.enter_context(tc.tile_pool(name="stage", bufs=6))
         banks = ctx.enter_context(tc.psum_pool(name="banks", bufs=6))
-        prev_banks = ctx.enter_context(tc.psum_pool(name="prev_banks", bufs=2))
+        diff_banks = ctx.enter_context(tc.psum_pool(name="diff_banks", bufs=1))
 
-        x_v_row0 = consts.tile([P, C], BF16)
-        nc.vector.memset(x_v_row0[:], 0.0)
-        nc.scalar.dma_start(out=x_v_row0[0:1, :], in_=x_v.rearrange("a b c -> (a b) c"))
+        x_v_rows = consts.tile([P, CHUNK], BF16)
+        nc.vector.memset(x_v_rows[:], 0.0)
 
         x_chunks = []
         for n in range(X_CHUNKS):
@@ -72,45 +71,69 @@ def tile_full_tmix_params_pb_v_kernel(
             nc.sync.dma_start(out=mix_loads[i][:], in_=mix_rows[:, :, cols])
 
         load_x_chunk(0)
+        nc.sync.dma_start(
+            out=x_v_rows[0:X_CHUNKS, :], in_=x_v.rearrange("a b (n c) -> (a b n) c", c=CHUNK)
+        )
         load_mix_and_grad(0)
         load_x_chunk(1)
         load_mix_and_grad(1)
         load_x_chunk(2)
         load_x_chunk(3)
 
-        ones = consts.tile([P, P], BF16)
-        nc.gpsimd.memset(ones[:], 1.0)
+        ident = consts.tile([P, P], BF16)
+        make_identity(nc, ident[:])
         shift_wide = consts.tile([P, P + 1], BF16)
         make_identity(nc, shift_wide[:, 1 : P + 1])
         shift = shift_wide[:, 0:P]
         nc.gpsimd.memset(shift.rearrange("k (s m) -> k s m", m=SEQ_PARTITIONS)[:, :, 0:1], 0.0)
+        minus_ident = consts.tile([P, P], BF16)
+        nc.vector.tensor_scalar_mul(out=minus_ident[:], in0=ident[:], scalar1=-1.0)
+        minus_shift = consts.tile([P, P], BF16)
+        nc.vector.tensor_scalar_mul(out=minus_shift[:], in0=shift, scalar1=-1.0)
 
         x_v_all = consts.tile([P, C], BF16)
         for n in range(X_CHUNKS):
-            cols = slice(n * CHUNK, (n + 1) * CHUNK)
             spread = banks.tile([P, CHUNK], F32, tag="bank")
             nc.tensor.matmul(
-                out=spread[:], lhsT=ones[:], rhs=x_v_row0[:, cols], start=True, stop=True
+                out=spread[:],
+                lhsT=ident[:, n : n + 1].to_broadcast([P, P]),
+                rhs=x_v_rows[:],
+                start=True,
+                stop=True,
             )
-            nc.scalar.copy(out=x_v_all[:, cols], in_=spread[:])
+            nc.scalar.copy(out=x_v_all[:, n * CHUNK : (n + 1) * CHUNK], in_=spread[:])
 
         xv_codes = keep.tile([P, C], U32, align_bytes=64)
         xv_scales = keep.tile([P, C], U8, align_bytes=64)
         dv_codes = keep.tile([P, CO], U32, align_bytes=64)
         dv_scales = keep.tile([P, CO], U8, align_bytes=64)
 
-        def shift_row3(n):
-            prev_row0 = prev_banks.tile([P, CHUNK], F32, tag="prev_row0")
-            nc.tensor.matmul(
-                out=prev_row0[:],
-                lhsT=shift,
-                rhs=x_chunks[n][:, PACK - 1, :],
-                start=True,
-                stop=True,
-            )
-            return prev_row0
+        def differences_on_tensor(n):
+            x_n = x_chunks[n]
+            diffs = []
+            for h in range(PIECES):
+                w = slice(h * PIECE, (h + 1) * PIECE)
+                diff = diff_banks.tile([P, TENSOR_ROWS, PIECE], F32, name="diff%d" % h)
+                nc.tensor.matmul(
+                    out=diff[:, 0, :], lhsT=ident[:], rhs=x_n[:, 0, w], start=True, stop=False
+                )
+                nc.tensor.matmul(
+                    out=diff[:, 0, :],
+                    lhsT=minus_shift[:],
+                    rhs=x_n[:, PACK - 1, w],
+                    start=False,
+                    stop=True,
+                )
+                nc.tensor.matmul(
+                    out=diff[:, 1, :], lhsT=ident[:], rhs=x_n[:, 1, w], start=True, stop=False
+                )
+                nc.tensor.matmul(
+                    out=diff[:, 1, :], lhsT=minus_ident[:], rhs=x_n[:, 0, w], start=False, stop=True
+                )
+                diffs.append(diff)
+            return diffs
 
-        def prepare_xv(n, prev_row0):
+        def prepare_xv(n, diffs):
             x_n = x_chunks[n]
             piece_cols = [slice(h * PIECE, (h + 1) * PIECE) for h in range(PIECES)]
             terms = []
@@ -123,29 +146,31 @@ def tile_full_tmix_params_pb_v_kernel(
             for h in range(PIECES):
                 w = piece_cols[h]
                 nc.vector.tensor_tensor(
-                    out=terms[h][:, 1:PACK, :],
-                    in0=x_n[:, 1:PACK, w],
-                    in1=x_n[:, 0 : PACK - 1, w],
+                    out=terms[h][:, TENSOR_ROWS:PACK, :],
+                    in0=x_n[:, TENSOR_ROWS:PACK, w],
+                    in1=x_n[:, TENSOR_ROWS - 1 : PACK - 1, w],
                     op=ALU.subtract,
-                )
-                nc.vector.tensor_tensor(
-                    out=terms[h][:, 0, :], in0=x_n[:, 0, w], in1=prev_row0[:, w], op=ALU.subtract
                 )
             for h in range(PIECES):
                 first = n * CHUNK + h * PIECE
+                x_v_piece = x_v_all[:, first : first + PIECE].unsqueeze(1)
                 nc.vector.tensor_tensor(
-                    out=terms[h][:],
-                    in0=terms[h][:],
-                    in1=x_v_all[:, first : first + PIECE]
-                    .unsqueeze(1)
-                    .to_broadcast([P, PACK, PIECE]),
+                    out=terms[h][:, 0:TENSOR_ROWS, :],
+                    in0=diffs[h][:],
+                    in1=x_v_piece.to_broadcast([P, TENSOR_ROWS, PIECE]),
+                    op=ALU.mult,
+                )
+                nc.vector.tensor_tensor(
+                    out=terms[h][:, TENSOR_ROWS:PACK, :],
+                    in0=terms[h][:, TENSOR_ROWS:PACK, :],
+                    in1=x_v_piece.to_broadcast([P, PACK - TENSOR_ROWS, PIECE]),
                     op=ALU.mult,
                 )
             for h in range(PIECES):
                 nc.vector.tensor_tensor(
-                    out=grouped[h][:].rearrange("p (r i) j -> p r j i", i=RUN),
-                    in0=terms[h][:].rearrange("p j (r i) -> p r j i", i=RUN),
-                    in1=x_n[:, :, piece_cols[h]].rearrange("p j (r i) -> p r j i", i=RUN),
+                    out=grouped[h][:],
+                    in0=terms[h][:].rearrange("p j w -> p w j"),
+                    in1=x_n[:, :, piece_cols[h]].rearrange("p j w -> p w j"),
                     op=ALU.subtract,
                 )
             for h in range(PIECES):
@@ -208,27 +233,24 @@ def tile_full_tmix_params_pb_v_kernel(
         def m_tiles_of(d):
             return range(d * M_TILES_PER_CHUNK, (d + 1) * M_TILES_PER_CHUNK)
 
-        prev_row0 = shift_row3(0)
-        prepare_xv(0, prev_row0)
-        prev_row0 = shift_row3(1)
+        diffs = differences_on_tensor(0)
+        prepare_xv(0, diffs)
+        diffs = differences_on_tensor(1)
         prepare_dv(0)
         for m in m_tiles_of(0):
             multiply_and_store(m, 0, 1, False)
-        prepare_xv(1, prev_row0)
+        prepare_xv(1, diffs)
+        diffs = differences_on_tensor(2)
         for m in m_tiles_of(0):
             multiply_and_store(m, 1, 1, False)
-        prepare_dv(1)
-        for m in m_tiles_of(1):
-            multiply_and_store(m, 0, 2, False)
-        prev_row0_of_2 = shift_row3(2)
-        prev_row0_of_3 = shift_row3(3)
-        for d in range(2, DV_CHUNKS):
+        for d in range(1, DV_CHUNKS):
             prepare_dv(d)
             for m in m_tiles_of(d):
                 multiply_and_store(m, 0, 2, False)
-        prepare_xv(2, prev_row0_of_2)
+        prepare_xv(2, diffs)
+        diffs = differences_on_tensor(3)
         for m in range(M_TILES):
             multiply_and_store(m, 2, 1, False)
-        prepare_xv(3, prev_row0_of_3)
+        prepare_xv(3, diffs)
         for m in range(M_TILES):
             multiply_and_store(m, 3, 1, True)

@@ -13,20 +13,29 @@ ALU = mybir.AluOpType
 
 P = 128
 PACK = 4
-TOKENS = P * PACK
-SEQ_PARTITIONS = 128 // PACK
+SEQS = 4
+SEQ = 128
+TOKENS = SEQS * SEQ
+WORDS = TOKENS // 2
 C = 2048
 CO = 2048
 CHUNK = 512
 PIECE = CHUNK // 2
 PIECES = CHUNK // PIECE
-TENSOR_ROWS = 2
+C_TILE = 128
+C_TILES = C // C_TILE
+PAIR = 2
+STEP_COLS = PAIR * C_TILE
+STEPS = C // STEP_COLS
+STEPS_PER_CHUNK = CHUNK // STEP_COLS
 M_TILE = 128
 X_CHUNKS = C // CHUNK
 DV_CHUNKS = CO // CHUNK
 M_TILES = CO // M_TILE
 M_TILES_PER_CHUNK = CHUNK // M_TILE
 LOAD_COLS = 2 * CHUNK
+BANKS = 8
+STEP_BANKS = 4
 
 FLOPS = 2 * TOKENS * CO * C
 BYTES = 2 * TOKENS * C + 2 * C + 4 * TOKENS * CO + 2 * TOKENS * CO + 4 * CO * C
@@ -36,7 +45,7 @@ def tile_full_tmix_params_pb_v_kernel(
     tc, x, x_v, W_v, v_hid, v2, v0, v_first, mix, grad_out, out
 ):
     nc = tc.nc
-    x_rows = x.rearrange("b (q j) c -> (b q) j c", j=PACK)
+    x_by_token = x.rearrange("b t c -> t b c")
     mix_rows = mix.rearrange("b (q j) c -> (b q) j c", j=PACK)
     grad_rows = grad_out.rearrange("b (q j) c -> (b q) j c", j=PACK)
 
@@ -45,17 +54,16 @@ def tile_full_tmix_params_pb_v_kernel(
         consts = ctx.enter_context(tc.tile_pool(name="consts", bufs=1))
         inputs = ctx.enter_context(tc.tile_pool(name="inputs", bufs=1))
         keep = ctx.enter_context(tc.tile_pool(name="keep", bufs=1))
-        work = ctx.enter_context(tc.tile_pool(name="work", bufs=2))
-        stage_pool = ctx.enter_context(tc.tile_pool(name="stage", bufs=6))
-        banks = ctx.enter_context(tc.psum_pool(name="banks", bufs=6))
-        diff_banks = ctx.enter_context(tc.psum_pool(name="diff_banks", bufs=1))
+        work = ctx.enter_context(tc.tile_pool(name="work", bufs=3))
+        stage_pool = ctx.enter_context(tc.tile_pool(name="stage", bufs=5))
+        psum = ctx.enter_context(tc.psum_pool(name="psum", bufs=1))
 
-        x_v_rows = consts.tile([P, CHUNK], BF16)
+        x_v_rows = consts.tile([P, P], BF16)
         nc.vector.memset(x_v_rows[:], 0.0)
 
         x_chunks = []
         for n in range(X_CHUNKS):
-            x_chunks.append(inputs.tile([P, PACK, CHUNK], BF16, name="x_chunk%d" % n))
+            x_chunks.append(inputs.tile([P, SEQS, CHUNK], BF16, name="x_chunk%d" % n))
         mix_loads = []
         grad_loads = []
         for i in range(CO // LOAD_COLS):
@@ -63,7 +71,9 @@ def tile_full_tmix_params_pb_v_kernel(
             grad_loads.append(inputs.tile([P, PACK, LOAD_COLS], BF16, name="grad_load%d" % i))
 
         def load_x_chunk(n):
-            nc.sync.dma_start(out=x_chunks[n][:], in_=x_rows[:, :, n * CHUNK : (n + 1) * CHUNK])
+            nc.sync.dma_start(
+                out=x_chunks[n][:], in_=x_by_token[:, :, n * CHUNK : (n + 1) * CHUNK]
+            )
 
         def load_mix_and_grad(i):
             cols = slice(i * LOAD_COLS, (i + 1) * LOAD_COLS)
@@ -72,146 +82,130 @@ def tile_full_tmix_params_pb_v_kernel(
 
         load_x_chunk(0)
         nc.sync.dma_start(
-            out=x_v_rows[0:X_CHUNKS, :], in_=x_v.rearrange("a b (n c) -> (a b n) c", c=CHUNK)
+            out=x_v_rows[0:C_TILES, :], in_=x_v.rearrange("a b (n c) -> (a b n) c", c=C_TILE)
         )
+        for n in range(1, X_CHUNKS):
+            load_x_chunk(n)
         load_mix_and_grad(0)
-        load_x_chunk(1)
         load_mix_and_grad(1)
-        load_x_chunk(2)
-        load_x_chunk(3)
 
         ident = consts.tile([P, P], BF16)
         make_identity(nc, ident[:])
+        ident_words = consts.tile([P, P], F32)
+        make_identity(nc, ident_words[:])
         shift_wide = consts.tile([P, P + 1], BF16)
         make_identity(nc, shift_wide[:, 1 : P + 1])
-        shift = shift_wide[:, 0:P]
-        nc.gpsimd.memset(shift.rearrange("k (s m) -> k s m", m=SEQ_PARTITIONS)[:, :, 0:1], 0.0)
-        minus_ident = consts.tile([P, P], BF16)
-        nc.vector.tensor_scalar_mul(out=minus_ident[:], in0=ident[:], scalar1=-1.0)
-        minus_shift = consts.tile([P, P], BF16)
-        nc.vector.tensor_scalar_mul(out=minus_shift[:], in0=shift, scalar1=-1.0)
+        nc.gpsimd.memset(shift_wide[:, 0:1], 0.0)
+        minus_prev = consts.tile([P, P], BF16)
+        nc.vector.tensor_tensor(
+            out=minus_prev[:], in0=ident[:], in1=shift_wide[:, 0:P], op=ALU.subtract
+        )
 
-        x_v_all = consts.tile([P, C], BF16)
-        for n in range(X_CHUNKS):
-            spread = banks.tile([P, CHUNK], F32, tag="bank")
-            nc.tensor.matmul(
-                out=spread[:],
-                lhsT=ident[:, n : n + 1].to_broadcast([P, P]),
-                rhs=x_v_rows[:],
-                start=True,
-                stop=True,
-            )
-            nc.scalar.copy(out=x_v_all[:, n * CHUNK : (n + 1) * CHUNK], in_=spread[:])
+        x_v_turned = psum.tile([P, P], BF16, tag="bank%d" % (BANKS - 1))
+        nc.tensor.transpose(x_v_turned[:], x_v_rows[:], ident[:])
+        x_v_cols = consts.tile([P, C_TILES], F32)
+        nc.vector.tensor_copy(out=x_v_cols[:], in_=x_v_turned[:, 0:C_TILES])
 
         xv_codes = keep.tile([P, C], U32, align_bytes=64)
         xv_scales = keep.tile([P, C], U8, align_bytes=64)
         dv_codes = keep.tile([P, CO], U32, align_bytes=64)
         dv_scales = keep.tile([P, CO], U8, align_bytes=64)
 
-        def differences_on_tensor(n):
-            x_n = x_chunks[n]
-            diffs = []
-            for h in range(PIECES):
-                w = slice(h * PIECE, (h + 1) * PIECE)
-                diff = diff_banks.tile([P, TENSOR_ROWS, PIECE], F32, name="diff%d" % h)
-                nc.tensor.matmul(
-                    out=diff[:, 0, :], lhsT=ident[:], rhs=x_n[:, 0, w], start=True, stop=False
-                )
-                nc.tensor.matmul(
-                    out=diff[:, 0, :],
-                    lhsT=minus_shift[:],
-                    rhs=x_n[:, PACK - 1, w],
-                    start=False,
-                    stop=True,
-                )
-                nc.tensor.matmul(
-                    out=diff[:, 1, :], lhsT=ident[:], rhs=x_n[:, 1, w], start=True, stop=False
-                )
-                nc.tensor.matmul(
-                    out=diff[:, 1, :], lhsT=minus_ident[:], rhs=x_n[:, 0, w], start=False, stop=True
-                )
-                diffs.append(diff)
-            return diffs
+        xv_turned = {}
+        xv_grouped = {}
+        dv_grouped = {}
 
-        def prepare_xv(n, diffs):
-            x_n = x_chunks[n]
-            piece_cols = [slice(h * PIECE, (h + 1) * PIECE) for h in range(PIECES)]
-            terms = []
-            grouped = []
-            for h in range(PIECES):
-                terms.append(work.tile([P, PACK, PIECE], F32, name="term%d" % h))
-                grouped.append(
-                    work.tile([P, PIECE, PACK], BF16, name="xv_grouped%d" % h, align_bytes=64)
+        def xv_by_channel(s):
+            x_n = x_chunks[s // STEPS_PER_CHUNK]
+            first = s % STEPS_PER_CHUNK * STEP_COLS
+            bank = s % 2 * STEP_BANKS
+            blocks = []
+            for e in range(PAIR):
+                for b in range(SEQS):
+                    cols = slice(first + e * C_TILE, first + (e + 1) * C_TILE)
+                    blocks.append((e, slice(b * SEQ, (b + 1) * SEQ), x_n[:, b, cols]))
+            x_t = psum.tile([P, PAIR, TOKENS], BF16, tag="bank%d" % bank)
+            for e, tokens, block in blocks:
+                nc.tensor.transpose(x_t[:, e, tokens], block, ident[:])
+            x_t_sb = work.tile([P, PAIR, TOKENS], BF16)
+            nc.scalar.copy(out=x_t_sb[:], in_=x_t[:])
+            diff_t = []
+            for e in range(PAIR):
+                diff_t.append(
+                    psum.tile([P, TOKENS], F32, tag="bank%d" % (bank + 1 + e), name="diff_t%d" % e)
                 )
-            for h in range(PIECES):
-                w = piece_cols[h]
-                nc.vector.tensor_tensor(
-                    out=terms[h][:, TENSOR_ROWS:PACK, :],
-                    in0=x_n[:, TENSOR_ROWS:PACK, w],
-                    in1=x_n[:, TENSOR_ROWS - 1 : PACK - 1, w],
-                    op=ALU.subtract,
+            for e, tokens, block in blocks:
+                nc.tensor.matmul(
+                    out=diff_t[e][:, tokens], lhsT=block, rhs=minus_prev[:], start=True, stop=True
                 )
-            for h in range(PIECES):
-                first = n * CHUNK + h * PIECE
-                x_v_piece = x_v_all[:, first : first + PIECE].unsqueeze(1)
-                nc.vector.tensor_tensor(
-                    out=terms[h][:, 0:TENSOR_ROWS, :],
-                    in0=diffs[h][:],
-                    in1=x_v_piece.to_broadcast([P, TENSOR_ROWS, PIECE]),
-                    op=ALU.mult,
+            xv_t = work.tile([P, PAIR, TOKENS], BF16)
+            for e in range(PAIR):
+                n = s * PAIR + e
+                nc.vector.scalar_tensor_tensor(
+                    out=xv_t[:, e, :],
+                    in0=diff_t[e][:],
+                    scalar=x_v_cols[:, n : n + 1],
+                    in1=x_t_sb[:, e, :],
+                    op0=ALU.mult,
+                    op1=ALU.subtract,
                 )
-                nc.vector.tensor_tensor(
-                    out=terms[h][:, TENSOR_ROWS:PACK, :],
-                    in0=terms[h][:, TENSOR_ROWS:PACK, :],
-                    in1=x_v_piece.to_broadcast([P, PACK - TENSOR_ROWS, PIECE]),
-                    op=ALU.mult,
-                )
-            for h in range(PIECES):
-                nc.vector.tensor_tensor(
-                    out=grouped[h][:],
-                    in0=terms[h][:].rearrange("p j w -> p w j"),
-                    in1=x_n[:, :, piece_cols[h]].rearrange("p j w -> p w j"),
-                    op=ALU.subtract,
-                )
-            for h in range(PIECES):
-                cols = slice(n * CHUNK + h * PIECE, n * CHUNK + (h + 1) * PIECE)
-                nc.vector.quantize_mx(
-                    out=xv_codes[:, cols].bitcast(E4M3_X4),
-                    scales=xv_scales[:, cols],
-                    in_=grouped[h][:].rearrange("p w j -> p (w j)"),
-                )
+            xv_turned[s] = xv_t
 
-        def prepare_dv(d):
+        def xv_by_token(s):
+            bank = s % 2 * STEP_BANKS + STEP_BANKS - 1
+            back = psum.tile([P, PAIR, 2, C_TILE], F32, tag="bank%d" % bank)
+            for e in range(PAIR):
+                words = xv_turned[s][:, e, :].bitcast(F32)
+                for u in range(2):
+                    nc.tensor.transpose(back[:, e, u, :], words[:, u:WORDS:2], ident_words[:])
+            grouped = work.tile([P, STEP_COLS * PACK], BF16, align_bytes=64)
+            nc.scalar.copy(
+                out=grouped[:].bitcast(F32).rearrange("p (e c u) -> p e c u", e=PAIR, u=2),
+                in_=back[:].rearrange("p e u c -> p e c u"),
+            )
+            xv_grouped[s] = grouped
+
+        def quantise_xv(s):
+            cols = slice(s * STEP_COLS, (s + 1) * STEP_COLS)
+            nc.vector.quantize_mx(
+                out=xv_codes[:, cols].bitcast(E4M3_X4),
+                scales=xv_scales[:, cols],
+                in_=xv_grouped[s][:],
+            )
+
+        def dv_product(d, h):
             mix_sb = mix_loads[d * CHUNK // LOAD_COLS]
             grad_sb = grad_loads[d * CHUNK // LOAD_COLS]
-            grouped = []
-            for h in range(PIECES):
-                first = d * CHUNK % LOAD_COLS + h * PIECE
-                grouped.append(
-                    work.tile([P, PIECE, PACK], BF16, name="dv_grouped%d" % h, align_bytes=64)
-                )
-                nc.vector.scalar_tensor_tensor(
-                    out=grouped[h][:],
-                    in0=mix_sb[:, :, first : first + PIECE].rearrange("p j w -> p w j"),
-                    scalar=1.0,
-                    in1=grad_sb[:, :, first : first + PIECE].rearrange("p j w -> p w j"),
-                    op0=ALU.subtract,
-                    op1=ALU.mult,
-                )
-            for h in range(PIECES):
-                cols = slice(d * CHUNK + h * PIECE, d * CHUNK + (h + 1) * PIECE)
-                nc.vector.quantize_mx(
-                    out=dv_codes[:, cols].bitcast(E5M2_X4),
-                    scales=dv_scales[:, cols],
-                    in_=grouped[h][:].rearrange("p w j -> p (w j)"),
-                )
+            first = d * CHUNK % LOAD_COLS + h * PIECE
+            grouped = work.tile([P, PIECE, PACK], BF16, name="dv_grouped%d" % h, align_bytes=64)
+            nc.vector.scalar_tensor_tensor(
+                out=grouped[:],
+                in0=mix_sb[:, :, first : first + PIECE].rearrange("p j w -> p w j"),
+                scalar=1.0,
+                in1=grad_sb[:, :, first : first + PIECE].rearrange("p j w -> p w j"),
+                op0=ALU.subtract,
+                op1=ALU.mult,
+            )
+            dv_grouped[(d, h)] = grouped
 
-        def multiply_and_store(m, first_chunk, chunks, vector_helps):
+        def quantise_dv(d, h):
+            cols = slice(d * CHUNK + h * PIECE, d * CHUNK + (h + 1) * PIECE)
+            nc.vector.quantize_mx(
+                out=dv_codes[:, cols].bitcast(E5M2_X4),
+                scales=dv_scales[:, cols],
+                in_=dv_grouped[(d, h)][:].rearrange("p w j -> p (w j)"),
+            )
+
+        dv_stages = [(dv_product, 0), (dv_product, 1), (quantise_dv, 0), (quantise_dv, 1)]
+
+        def multiply_and_store(m):
             rows = slice(m * M_TILE, (m + 1) * M_TILE)
-            stage = stage_pool.tile([P, chunks * CHUNK], F32, tag="stage%d" % chunks)
-            for i in range(chunks):
-                cols = slice((first_chunk + i) * CHUNK, (first_chunk + i + 1) * CHUNK)
-                product = banks.tile([P, CHUNK], F32, tag="bank")
+            stage = stage_pool.tile([P, C], F32)
+            for n in range(X_CHUNKS):
+                cols = slice(n * CHUNK, (n + 1) * CHUNK)
+                product = psum.tile(
+                    [P, CHUNK], F32, tag="bank%d" % ((m * X_CHUNKS + n) % BANKS)
+                )
                 nc.tensor.matmul_mx(
                     out=product[:],
                     lhsT=dv_codes[:, rows].bitcast(E5M2_X4),
@@ -221,36 +215,25 @@ def tile_full_tmix_params_pb_v_kernel(
                     start=True,
                     stop=True,
                 )
-                stage_cols = stage[:, i * CHUNK : (i + 1) * CHUNK]
-                if vector_helps and m % 2 == 1:
-                    nc.vector.tensor_copy(out=stage_cols, in_=product[:])
+                if n == X_CHUNKS - 1:
+                    nc.vector.tensor_copy(out=stage[:, cols], in_=product[:])
                 else:
-                    nc.scalar.copy(out=stage_cols, in_=product[:])
-            nc.sync.dma_start(
-                out=out[rows, first_chunk * CHUNK : (first_chunk + chunks) * CHUNK], in_=stage[:]
-            )
+                    nc.scalar.copy(out=stage[:, cols], in_=product[:])
+            nc.sync.dma_start(out=out[rows, :], in_=stage[:])
 
-        def m_tiles_of(d):
-            return range(d * M_TILES_PER_CHUNK, (d + 1) * M_TILES_PER_CHUNK)
-
-        diffs = differences_on_tensor(0)
-        prepare_xv(0, diffs)
-        diffs = differences_on_tensor(1)
-        prepare_dv(0)
-        for m in m_tiles_of(0):
-            multiply_and_store(m, 0, 1, False)
-        prepare_xv(1, diffs)
-        diffs = differences_on_tensor(2)
-        for m in m_tiles_of(0):
-            multiply_and_store(m, 1, 1, False)
-        for d in range(1, DV_CHUNKS):
-            prepare_dv(d)
-            for m in m_tiles_of(d):
-                multiply_and_store(m, 0, 2, False)
-        prepare_xv(2, diffs)
-        diffs = differences_on_tensor(3)
+        for s in range(STEPS + 2):
+            if s < STEPS:
+                xv_by_channel(s)
+            if 1 <= s <= STEPS:
+                xv_by_token(s - 1)
+            if s >= 2:
+                quantise_xv(s - 2)
+            if s >= STEPS + 2 - len(dv_stages):
+                stage_fn, h = dv_stages[s - (STEPS + 2 - len(dv_stages))]
+                stage_fn(0, h)
         for m in range(M_TILES):
-            multiply_and_store(m, 2, 1, False)
-        prepare_xv(3, diffs)
-        for m in range(M_TILES):
-            multiply_and_store(m, 3, 1, True)
+            multiply_and_store(m)
+            d = m // M_TILES_PER_CHUNK + 1
+            if d < DV_CHUNKS:
+                stage_fn, h = dv_stages[m % M_TILES_PER_CHUNK]
+                stage_fn(d, h)

@@ -36,6 +36,8 @@ M_TILES_PER_CHUNK = CHUNK // M_TILE
 LOAD_COLS = 2 * CHUNK
 BANKS = 8
 STEP_BANKS = 4
+FIRST_DV_STEP = 5
+EARLY_M_TILES = 2
 
 FLOPS = 2 * TOKENS * CO * C
 BYTES = 2 * TOKENS * C + 2 * C + 4 * TOKENS * CO + 2 * TOKENS * CO + 4 * CO * C
@@ -111,30 +113,38 @@ def tile_full_tmix_params_pb_v_kernel(
         dv_codes = keep.tile([P, CO], U32, align_bytes=64)
         dv_scales = keep.tile([P, CO], U8, align_bytes=64)
 
+        x_turned = {}
         xv_turned = {}
         xv_grouped = {}
         dv_grouped = {}
 
-        def xv_by_channel(s):
+        def blocks_of(s):
             x_n = x_chunks[s // STEPS_PER_CHUNK]
             first = s % STEPS_PER_CHUNK * STEP_COLS
-            bank = s % 2 * STEP_BANKS
             blocks = []
             for e in range(PAIR):
                 for b in range(SEQS):
                     cols = slice(first + e * C_TILE, first + (e + 1) * C_TILE)
                     blocks.append((e, slice(b * SEQ, (b + 1) * SEQ), x_n[:, b, cols]))
-            x_t = psum.tile([P, PAIR, TOKENS], BF16, tag="bank%d" % bank)
-            for e, tokens, block in blocks:
+            return blocks
+
+        def turn_x(s):
+            x_t = psum.tile([P, PAIR, TOKENS], BF16, tag="bank%d" % (s % 2 * STEP_BANKS))
+            for e, tokens, block in blocks_of(s):
                 nc.tensor.transpose(x_t[:, e, tokens], block, ident[:])
             x_t_sb = work.tile([P, PAIR, TOKENS], BF16)
             nc.scalar.copy(out=x_t_sb[:], in_=x_t[:])
+            x_turned[s] = x_t_sb
+
+        def xv_by_channel(s):
+            bank = s % 2 * STEP_BANKS
+            x_t_sb = x_turned[s]
             diff_t = []
             for e in range(PAIR):
                 diff_t.append(
                     psum.tile([P, TOKENS], F32, tag="bank%d" % (bank + 1 + e), name="diff_t%d" % e)
                 )
-            for e, tokens, block in blocks:
+            for e, tokens, block in blocks_of(s):
                 nc.tensor.matmul(
                     out=diff_t[e][:, tokens], lhsT=block, rhs=minus_prev[:], start=True, stop=True
                 )
@@ -198,10 +208,15 @@ def tile_full_tmix_params_pb_v_kernel(
 
         dv_stages = [(dv_product, 0), (dv_product, 1), (quantise_dv, 0), (quantise_dv, 1)]
 
-        def multiply_and_store(m):
+        stages = {}
+
+        def multiply_and_store(m, first_chunk, chunks):
             rows = slice(m * M_TILE, (m + 1) * M_TILE)
-            stage = stage_pool.tile([P, C], F32)
-            for n in range(X_CHUNKS):
+            if m not in stages:
+                stage = stage_pool.tile([P, C], F32)
+                stages[m] = stage
+            stage = stages[m]
+            for n in range(first_chunk, first_chunk + chunks):
                 cols = slice(n * CHUNK, (n + 1) * CHUNK)
                 product = psum.tile(
                     [P, CHUNK], F32, tag="bank%d" % ((m * X_CHUNKS + n) % BANKS)
@@ -215,24 +230,32 @@ def tile_full_tmix_params_pb_v_kernel(
                     start=True,
                     stop=True,
                 )
-                if n == X_CHUNKS - 1:
+                if n % X_CHUNKS == 1:
                     nc.vector.tensor_copy(out=stage[:, cols], in_=product[:])
                 else:
                     nc.scalar.copy(out=stage[:, cols], in_=product[:])
-            nc.sync.dma_start(out=out[rows, :], in_=stage[:])
+            cols = slice(first_chunk * CHUNK, (first_chunk + chunks) * CHUNK)
+            nc.sync.dma_start(out=out[rows, cols], in_=stage[:, cols])
 
         for s in range(STEPS + 2):
             if s < STEPS:
+                turn_x(s)
+            if s >= 2:
+                xv_by_token(s - 2)
+            if s < STEPS:
                 xv_by_channel(s)
-            if 1 <= s <= STEPS:
-                xv_by_token(s - 1)
             if s >= 2:
                 quantise_xv(s - 2)
-            if s >= STEPS + 2 - len(dv_stages):
-                stage_fn, h = dv_stages[s - (STEPS + 2 - len(dv_stages))]
+            if 0 <= s - FIRST_DV_STEP < len(dv_stages):
+                stage_fn, h = dv_stages[s - FIRST_DV_STEP]
                 stage_fn(0, h)
+            if s >= STEPS:
+                multiply_and_store(s - STEPS, 0, X_CHUNKS - 1)
+        for m in range(EARLY_M_TILES):
+            multiply_and_store(m, X_CHUNKS - 1, 1)
         for m in range(M_TILES):
-            multiply_and_store(m)
+            if m >= EARLY_M_TILES:
+                multiply_and_store(m, 0, X_CHUNKS)
             d = m // M_TILES_PER_CHUNK + 1
             if d < DV_CHUNKS:
                 stage_fn, h = dv_stages[m % M_TILES_PER_CHUNK]

@@ -16,7 +16,6 @@ PACK = 4
 SEQS = 4
 SEQ = 128
 TOKENS = SEQS * SEQ
-WORDS = TOKENS // 2
 C = 2048
 CO = 2048
 CHUNK = 512
@@ -36,6 +35,8 @@ M_TILES_PER_CHUNK = CHUNK // M_TILE
 LOAD_COLS = 2 * CHUNK
 BANKS = 8
 STEP_BANKS = 4
+WARM_UP_MATMULS = 4
+KEEP_WARM_COLS = 320
 FIRST_DV_STEP = 5
 EARLY_M_TILES = 2
 
@@ -91,6 +92,18 @@ def tile_full_tmix_params_pb_v_kernel(
         load_mix_and_grad(0)
         load_mix_and_grad(1)
 
+        zeros = consts.tile([P, CHUNK], BF16)
+        nc.vector.memset(zeros[:], 0.0)
+
+        def idle_matmul(bank, width):
+            nc.tensor.matmul(
+                out=bank[:, 0:width], lhsT=zeros[:, 0:P], rhs=zeros[:, 0:width], start=True, stop=True
+            )
+
+        for i in range(WARM_UP_MATMULS):
+            idle_bank = psum.tile([P, CHUNK], F32, tag="bank%d" % (1 + i % 2))
+            idle_matmul(idle_bank, CHUNK)
+
         ident = consts.tile([P, P], BF16)
         make_identity(nc, ident[:])
         ident_words = consts.tile([P, P], F32)
@@ -102,6 +115,20 @@ def tile_full_tmix_params_pb_v_kernel(
         nc.vector.tensor_tensor(
             out=minus_prev[:], in0=ident[:], in1=shift_wide[:, 0:P], op=ALU.subtract
         )
+
+        def in_word_order(matrix, name):
+            permuted = consts.tile([P, P], BF16, name=name)
+            nc.vector.tensor_copy(
+                out=permuted[:].rearrange("k (u q e) -> k u q e", u=2, e=2),
+                in_=matrix.rearrange("k (q u e) -> k u q e", u=2, e=2),
+            )
+            return permuted
+
+        ident_ordered = in_word_order(ident[:], "ident_ordered")
+        minus_prev_ordered = in_word_order(minus_prev[:], "minus_prev_ordered")
+
+        def tokens_of(turned, b):
+            return turned.rearrange("c (u b j) -> c u b j", u=2, b=SEQS)[:, :, b, :]
 
         x_v_turned = psum.tile([P, P], BF16, tag="bank%d" % (BANKS - 1))
         nc.tensor.transpose(x_v_turned[:], x_v_rows[:], ident[:])
@@ -125,13 +152,13 @@ def tile_full_tmix_params_pb_v_kernel(
             for e in range(PAIR):
                 for b in range(SEQS):
                     cols = slice(first + e * C_TILE, first + (e + 1) * C_TILE)
-                    blocks.append((e, slice(b * SEQ, (b + 1) * SEQ), x_n[:, b, cols]))
+                    blocks.append((e, b, x_n[:, b, cols]))
             return blocks
 
         def turn_x(s):
             x_t = psum.tile([P, PAIR, TOKENS], BF16, tag="bank%d" % (s % 2 * STEP_BANKS))
-            for e, tokens, block in blocks_of(s):
-                nc.tensor.transpose(x_t[:, e, tokens], block, ident[:])
+            for e, b, block in blocks_of(s):
+                nc.tensor.transpose(tokens_of(x_t[:, e, :], b), block, ident_ordered[:])
             x_t_sb = work.tile([P, PAIR, TOKENS], BF16)
             nc.scalar.copy(out=x_t_sb[:], in_=x_t[:])
             x_turned[s] = x_t_sb
@@ -144,9 +171,14 @@ def tile_full_tmix_params_pb_v_kernel(
                 diff_t.append(
                     psum.tile([P, TOKENS], F32, tag="bank%d" % (bank + 1 + e), name="diff_t%d" % e)
                 )
-            for e, tokens, block in blocks_of(s):
+            idle_matmul(diff_t[0], KEEP_WARM_COLS)
+            for e, b, block in blocks_of(s):
                 nc.tensor.matmul(
-                    out=diff_t[e][:, tokens], lhsT=block, rhs=minus_prev[:], start=True, stop=True
+                    out=tokens_of(diff_t[e][:], b),
+                    lhsT=block,
+                    rhs=minus_prev_ordered[:],
+                    start=True,
+                    stop=True,
                 )
             xv_t = work.tile([P, PAIR, TOKENS], BF16)
             for e in range(PAIR):
@@ -167,7 +199,9 @@ def tile_full_tmix_params_pb_v_kernel(
             for e in range(PAIR):
                 words = xv_turned[s][:, e, :].bitcast(F32)
                 for u in range(2):
-                    nc.tensor.transpose(back[:, e, u, :], words[:, u:WORDS:2], ident_words[:])
+                    nc.tensor.transpose(
+                        back[:, e, u, :], words[:, u * P : (u + 1) * P], ident_words[:]
+                    )
             grouped = work.tile([P, STEP_COLS * PACK], BF16, align_bytes=64)
             nc.scalar.copy(
                 out=grouped[:].bitcast(F32).rearrange("p (e c u) -> p e c u", e=PAIR, u=2),

@@ -20,7 +20,6 @@ C = 2048
 CO = 2048
 CHUNK = 512
 PIECE = CHUNK // 2
-PIECES = CHUNK // PIECE
 C_TILE = 128
 C_TILES = C // C_TILE
 PAIR = 2
@@ -29,15 +28,14 @@ STEPS = C // STEP_COLS
 STEPS_PER_CHUNK = CHUNK // STEP_COLS
 M_TILE = 128
 X_CHUNKS = C // CHUNK
-DV_CHUNKS = CO // CHUNK
 M_TILES = CO // M_TILE
-M_TILES_PER_CHUNK = CHUNK // M_TILE
-LOAD_COLS = 2 * CHUNK
+DV_LOAD_ENDS = [PIECE, 2 * CHUNK, CO]
+DV_PIECES = CO // PIECE
+M_TILES_PER_PIECE = PIECE // M_TILE
 BANKS = 8
 STEP_BANKS = 4
 WARM_UP_MATMULS = 4
 KEEP_WARM_COLS = 320
-FIRST_DV_STEP = 5
 EARLY_M_TILES = 2
 
 FLOPS = 2 * TOKENS * CO * C
@@ -69,9 +67,10 @@ def tile_full_tmix_params_pb_v_kernel(
             x_chunks.append(inputs.tile([P, SEQS, CHUNK], BF16, name="x_chunk%d" % n))
         mix_loads = []
         grad_loads = []
-        for i in range(CO // LOAD_COLS):
-            mix_loads.append(inputs.tile([P, PACK, LOAD_COLS], F32, name="mix_load%d" % i))
-            grad_loads.append(inputs.tile([P, PACK, LOAD_COLS], BF16, name="grad_load%d" % i))
+        for i in range(len(DV_LOAD_ENDS)):
+            width = DV_LOAD_ENDS[i] - ([0] + DV_LOAD_ENDS)[i]
+            mix_loads.append(inputs.tile([P, PACK, width], F32, name="mix_load%d" % i))
+            grad_loads.append(inputs.tile([P, PACK, width], BF16, name="grad_load%d" % i))
 
         def load_x_chunk(n):
             nc.sync.dma_start(
@@ -79,7 +78,7 @@ def tile_full_tmix_params_pb_v_kernel(
             )
 
         def load_mix_and_grad(i):
-            cols = slice(i * LOAD_COLS, (i + 1) * LOAD_COLS)
+            cols = slice(([0] + DV_LOAD_ENDS)[i], DV_LOAD_ENDS[i])
             nc.sync.dma_start(out=grad_loads[i][:], in_=grad_rows[:, :, cols])
             nc.sync.dma_start(out=mix_loads[i][:], in_=mix_rows[:, :, cols])
 
@@ -87,10 +86,11 @@ def tile_full_tmix_params_pb_v_kernel(
         nc.sync.dma_start(
             out=x_v_rows[0:C_TILES, :], in_=x_v.rearrange("a b (n c) -> (a b n) c", c=C_TILE)
         )
+        load_mix_and_grad(0)
         for n in range(1, X_CHUNKS):
             load_x_chunk(n)
-        load_mix_and_grad(0)
-        load_mix_and_grad(1)
+        for i in range(1, len(DV_LOAD_ENDS)):
+            load_mix_and_grad(i)
 
         zeros = consts.tile([P, CHUNK], BF16)
         nc.vector.memset(zeros[:], 0.0)
@@ -217,30 +217,29 @@ def tile_full_tmix_params_pb_v_kernel(
                 in_=xv_grouped[s][:],
             )
 
-        def dv_product(d, h):
-            mix_sb = mix_loads[d * CHUNK // LOAD_COLS]
-            grad_sb = grad_loads[d * CHUNK // LOAD_COLS]
-            first = d * CHUNK % LOAD_COLS + h * PIECE
-            grouped = work.tile([P, PIECE, PACK], BF16, name="dv_grouped%d" % h, align_bytes=64)
+        def dv_product(k):
+            i = min([i for i in range(len(DV_LOAD_ENDS)) if k * PIECE < DV_LOAD_ENDS[i]])
+            first = k * PIECE - ([0] + DV_LOAD_ENDS)[i]
+            grouped = work.tile(
+                [P, PIECE, PACK], BF16, name="dv_grouped%d" % (k % 2), align_bytes=64
+            )
             nc.vector.scalar_tensor_tensor(
                 out=grouped[:],
-                in0=mix_sb[:, :, first : first + PIECE].rearrange("p j w -> p w j"),
+                in0=mix_loads[i][:, :, first : first + PIECE].rearrange("p j w -> p w j"),
                 scalar=1.0,
-                in1=grad_sb[:, :, first : first + PIECE].rearrange("p j w -> p w j"),
+                in1=grad_loads[i][:, :, first : first + PIECE].rearrange("p j w -> p w j"),
                 op0=ALU.subtract,
                 op1=ALU.mult,
             )
-            dv_grouped[(d, h)] = grouped
+            dv_grouped[k] = grouped
 
-        def quantise_dv(d, h):
-            cols = slice(d * CHUNK + h * PIECE, d * CHUNK + (h + 1) * PIECE)
+        def quantise_dv(k):
+            cols = slice(k * PIECE, (k + 1) * PIECE)
             nc.vector.quantize_mx(
                 out=dv_codes[:, cols].bitcast(E5M2_X4),
                 scales=dv_scales[:, cols],
-                in_=dv_grouped[(d, h)][:].rearrange("p w j -> p (w j)"),
+                in_=dv_grouped[k][:].rearrange("p w j -> p (w j)"),
             )
-
-        dv_stages = [(dv_product, 0), (dv_product, 1), (quantise_dv, 0), (quantise_dv, 1)]
 
         stages = {}
 
@@ -271,6 +270,7 @@ def tile_full_tmix_params_pb_v_kernel(
             cols = slice(first_chunk * CHUNK, (first_chunk + chunks) * CHUNK)
             nc.sync.dma_start(out=out[rows, cols], in_=stage[:, cols])
 
+        dv_product(0)
         for s in range(STEPS + 2):
             if s < STEPS:
                 turn_x(s)
@@ -278,19 +278,23 @@ def tile_full_tmix_params_pb_v_kernel(
                 xv_by_token(s - 2)
             if s < STEPS:
                 xv_by_channel(s)
+            if s == 0:
+                quantise_dv(0)
             if s >= 2:
                 quantise_xv(s - 2)
-            if 0 <= s - FIRST_DV_STEP < len(dv_stages):
-                stage_fn, h = dv_stages[s - FIRST_DV_STEP]
-                stage_fn(0, h)
+            if s == STEPS + 1:
+                quantise_dv(1)
             if s >= STEPS:
                 multiply_and_store(s - STEPS, 0, X_CHUNKS - 1)
+            if s == STEPS:
+                dv_product(1)
         for m in range(EARLY_M_TILES):
             multiply_and_store(m, X_CHUNKS - 1, 1)
         for m in range(M_TILES):
             if m >= EARLY_M_TILES:
                 multiply_and_store(m, 0, X_CHUNKS)
-            d = m // M_TILES_PER_CHUNK + 1
-            if d < DV_CHUNKS:
-                stage_fn, h = dv_stages[m % M_TILES_PER_CHUNK]
-                stage_fn(d, h)
+            k = m // M_TILES_PER_PIECE + 2
+            if k < DV_PIECES and m % M_TILES_PER_PIECE == 0:
+                dv_product(k)
+            if k < DV_PIECES and m % M_TILES_PER_PIECE == 1:
+                quantise_dv(k)

@@ -36,6 +36,7 @@ BANKS = 8
 STEP_BANKS = 4
 WARM_UP_MATMULS = 4
 KEEP_WARM_COLS = 320
+FIRST_DV_STEP = 2
 EARLY_M_TILES = 2
 
 FLOPS = 2 * TOKENS * CO * C
@@ -86,8 +87,9 @@ def tile_full_tmix_params_pb_v_kernel(
         nc.sync.dma_start(
             out=x_v_rows[0:C_TILES, :], in_=x_v.rearrange("a b (n c) -> (a b n) c", c=C_TILE)
         )
+        load_x_chunk(1)
         load_mix_and_grad(0)
-        for n in range(1, X_CHUNKS):
+        for n in range(2, X_CHUNKS):
             load_x_chunk(n)
         for i in range(1, len(DV_LOAD_ENDS)):
             load_mix_and_grad(i)
@@ -217,21 +219,22 @@ def tile_full_tmix_params_pb_v_kernel(
                 in_=xv_grouped[s][:],
             )
 
-        def dv_product(k):
+        def dv_product(k, first_col, width):
             i = min([i for i in range(len(DV_LOAD_ENDS)) if k * PIECE < DV_LOAD_ENDS[i]])
-            first = k * PIECE - ([0] + DV_LOAD_ENDS)[i]
-            grouped = work.tile(
-                [P, PIECE, PACK], BF16, name="dv_grouped%d" % (k % 2), align_bytes=64
-            )
+            first = k * PIECE - ([0] + DV_LOAD_ENDS)[i] + first_col
+            if k not in dv_grouped:
+                grouped = work.tile(
+                    [P, PIECE, PACK], BF16, name="dv_grouped%d" % (k % 2), align_bytes=64
+                )
+                dv_grouped[k] = grouped
             nc.vector.scalar_tensor_tensor(
-                out=grouped[:],
-                in0=mix_loads[i][:, :, first : first + PIECE].rearrange("p j w -> p w j"),
+                out=dv_grouped[k][:, first_col : first_col + width, :],
+                in0=mix_loads[i][:, :, first : first + width].rearrange("p j w -> p w j"),
                 scalar=1.0,
-                in1=grad_loads[i][:, :, first : first + PIECE].rearrange("p j w -> p w j"),
+                in1=grad_loads[i][:, :, first : first + width].rearrange("p j w -> p w j"),
                 op0=ALU.subtract,
                 op1=ALU.mult,
             )
-            dv_grouped[k] = grouped
 
         def quantise_dv(k):
             cols = slice(k * PIECE, (k + 1) * PIECE)
@@ -270,7 +273,6 @@ def tile_full_tmix_params_pb_v_kernel(
             cols = slice(first_chunk * CHUNK, (first_chunk + chunks) * CHUNK)
             nc.sync.dma_start(out=out[rows, cols], in_=stage[:, cols])
 
-        dv_product(0)
         for s in range(STEPS + 2):
             if s < STEPS:
                 turn_x(s)
@@ -278,16 +280,18 @@ def tile_full_tmix_params_pb_v_kernel(
                 xv_by_token(s - 2)
             if s < STEPS:
                 xv_by_channel(s)
-            if s == 0:
-                quantise_dv(0)
             if s >= 2:
                 quantise_xv(s - 2)
+            if 0 <= s - FIRST_DV_STEP < M_TILES_PER_PIECE:
+                dv_product(0, (s - FIRST_DV_STEP) * M_TILE, M_TILE)
+            if s == FIRST_DV_STEP + M_TILES_PER_PIECE:
+                quantise_dv(0)
             if s == STEPS + 1:
                 quantise_dv(1)
             if s >= STEPS:
                 multiply_and_store(s - STEPS, 0, X_CHUNKS - 1)
             if s == STEPS:
-                dv_product(1)
+                dv_product(1, 0, PIECE)
         for m in range(EARLY_M_TILES):
             multiply_and_store(m, X_CHUNKS - 1, 1)
         for m in range(M_TILES):
@@ -295,6 +299,6 @@ def tile_full_tmix_params_pb_v_kernel(
                 multiply_and_store(m, 0, X_CHUNKS)
             k = m // M_TILES_PER_PIECE + 2
             if k < DV_PIECES and m % M_TILES_PER_PIECE == 0:
-                dv_product(k)
+                dv_product(k, 0, PIECE)
             if k < DV_PIECES and m % M_TILES_PER_PIECE == 1:
                 quantise_dv(k)

@@ -35,7 +35,6 @@ M_TILES_PER_PIECE = PIECE // M_TILE
 BANKS = 8
 STEP_BANKS = 4
 WARM_UP_MATMULS = 4
-KEEP_WARM_COLS = 320
 FIRST_DV_STEP = 2
 EARLY_M_TILES = 2
 
@@ -173,7 +172,6 @@ def tile_full_tmix_params_pb_v_kernel(
                 diff_t.append(
                     psum.tile([P, TOKENS], F32, tag="bank%d" % (bank + 1 + e), name="diff_t%d" % e)
                 )
-            idle_matmul(diff_t[0], KEEP_WARM_COLS)
             for e, b, block in blocks_of(s):
                 nc.tensor.matmul(
                     out=tokens_of(diff_t[e][:], b),

@@ -29,7 +29,10 @@ STEPS_PER_CHUNK = CHUNK // STEP_COLS
 M_TILE = 128
 X_CHUNKS = C // CHUNK
 M_TILES = CO // M_TILE
-DV_LOAD_ENDS = [PIECE, 2 * CHUNK, CO]
+X_LOAD_ENDS = [CHUNK, 2 * CHUNK, C]
+GRAD_LOAD_ENDS = [PIECE, CO]
+MIX_LOAD_ENDS = [PIECE, 2 * CHUNK, CO]
+LOAD_ORDER = ["x0", "x_v", "x1", "grad0", "mix0", "x2", "grad1", "mix1", "mix2"]
 DV_PIECES = CO // PIECE
 M_TILES_PER_PIECE = PIECE // M_TILE
 BANKS = 8
@@ -62,36 +65,36 @@ def tile_full_tmix_params_pb_v_kernel(
         x_v_rows = consts.tile([P, P], BF16)
         nc.vector.memset(x_v_rows[:], 0.0)
 
-        x_chunks = []
-        for n in range(X_CHUNKS):
-            x_chunks.append(inputs.tile([P, SEQS, CHUNK], BF16, name="x_chunk%d" % n))
-        mix_loads = []
-        grad_loads = []
-        for i in range(len(DV_LOAD_ENDS)):
-            width = DV_LOAD_ENDS[i] - ([0] + DV_LOAD_ENDS)[i]
-            mix_loads.append(inputs.tile([P, PACK, width], F32, name="mix_load%d" % i))
-            grad_loads.append(inputs.tile([P, PACK, width], BF16, name="grad_load%d" % i))
+        def tiles_for(ends, dtype, name):
+            tiles = []
+            for i in range(len(ends)):
+                width = ends[i] - ([0] + ends)[i]
+                tiles.append(inputs.tile([P, PACK, width], dtype, name="%s%d" % (name, i)))
+            return tiles
 
-        def load_x_chunk(n):
-            nc.sync.dma_start(
-                out=x_chunks[n][:], in_=x_by_token[:, :, n * CHUNK : (n + 1) * CHUNK]
-            )
+        x_loads = tiles_for(X_LOAD_ENDS, BF16, "x_load")
+        grad_loads = tiles_for(GRAD_LOAD_ENDS, BF16, "grad_load")
+        mix_loads = tiles_for(MIX_LOAD_ENDS, F32, "mix_load")
 
-        def load_mix_and_grad(i):
-            cols = slice(([0] + DV_LOAD_ENDS)[i], DV_LOAD_ENDS[i])
-            nc.sync.dma_start(out=grad_loads[i][:], in_=grad_rows[:, :, cols])
-            nc.sync.dma_start(out=mix_loads[i][:], in_=mix_rows[:, :, cols])
+        def load(tiles, ends, i, rows):
+            nc.sync.dma_start(out=tiles[i][:], in_=rows[:, :, ([0] + ends)[i] : ends[i]])
 
-        load_x_chunk(0)
-        nc.sync.dma_start(
-            out=x_v_rows[0:C_TILES, :], in_=x_v.rearrange("a b (n c) -> (a b n) c", c=C_TILE)
-        )
-        load_x_chunk(1)
-        load_mix_and_grad(0)
-        for n in range(2, X_CHUNKS):
-            load_x_chunk(n)
-        for i in range(1, len(DV_LOAD_ENDS)):
-            load_mix_and_grad(i)
+        def columns_of(tiles, ends, first_col, width):
+            i = min([i for i in range(len(ends)) if first_col < ends[i]])
+            first = first_col - ([0] + ends)[i]
+            return tiles[i][:, :, first : first + width]
+
+        for what in LOAD_ORDER:
+            if what == "x_v":
+                nc.sync.dma_start(
+                    out=x_v_rows[0:C_TILES, :], in_=x_v.rearrange("a b (n c) -> (a b n) c", c=C_TILE)
+                )
+            elif what.startswith("x"):
+                load(x_loads, X_LOAD_ENDS, int(what[1:]), x_by_token)
+            elif what.startswith("grad"):
+                load(grad_loads, GRAD_LOAD_ENDS, int(what[4:]), grad_rows)
+            else:
+                load(mix_loads, MIX_LOAD_ENDS, int(what[3:]), mix_rows)
 
         zeros = consts.tile([P, CHUNK], BF16)
         nc.vector.memset(zeros[:], 0.0)
@@ -147,13 +150,11 @@ def tile_full_tmix_params_pb_v_kernel(
         dv_grouped = {}
 
         def blocks_of(s):
-            x_n = x_chunks[s // STEPS_PER_CHUNK]
-            first = s % STEPS_PER_CHUNK * STEP_COLS
             blocks = []
             for e in range(PAIR):
+                x_tile = columns_of(x_loads, X_LOAD_ENDS, (s * PAIR + e) * C_TILE, C_TILE)
                 for b in range(SEQS):
-                    cols = slice(first + e * C_TILE, first + (e + 1) * C_TILE)
-                    blocks.append((e, b, x_n[:, b, cols]))
+                    blocks.append((e, b, x_tile[:, b, :]))
             return blocks
 
         def turn_x(s):
@@ -218,8 +219,7 @@ def tile_full_tmix_params_pb_v_kernel(
             )
 
         def dv_product(k, first_col, width):
-            i = min([i for i in range(len(DV_LOAD_ENDS)) if k * PIECE < DV_LOAD_ENDS[i]])
-            first = k * PIECE - ([0] + DV_LOAD_ENDS)[i] + first_col
+            first = k * PIECE + first_col
             if k not in dv_grouped:
                 grouped = work.tile(
                     [P, PIECE, PACK], BF16, name="dv_grouped%d" % (k % 2), align_bytes=64
@@ -227,9 +227,9 @@ def tile_full_tmix_params_pb_v_kernel(
                 dv_grouped[k] = grouped
             nc.vector.scalar_tensor_tensor(
                 out=dv_grouped[k][:, first_col : first_col + width, :],
-                in0=mix_loads[i][:, :, first : first + width].rearrange("p j w -> p w j"),
+                in0=columns_of(mix_loads, MIX_LOAD_ENDS, first, width).rearrange("p j w -> p w j"),
                 scalar=1.0,
-                in1=grad_loads[i][:, :, first : first + width].rearrange("p j w -> p w j"),
+                in1=columns_of(grad_loads, GRAD_LOAD_ENDS, first, width).rearrange("p j w -> p w j"),
                 op0=ALU.subtract,
                 op1=ALU.mult,
             )

@@ -39,6 +39,7 @@ BANKS = 8
 STEP_BANKS = 4
 WARM_UP_MATMULS = 4
 FIRST_DV_STEP = 2
+PAIRS_FROM = 8
 EARLY_M_TILES = 2
 
 FLOPS = 2 * TOKENS * CO * C
@@ -60,6 +61,7 @@ def tile_full_tmix_params_pb_v_kernel(
         keep = ctx.enter_context(tc.tile_pool(name="keep", bufs=1))
         work = ctx.enter_context(tc.tile_pool(name="work", bufs=3))
         stage_pool = ctx.enter_context(tc.tile_pool(name="stage", bufs=5))
+        pair_pool = ctx.enter_context(tc.tile_pool(name="pair", bufs=3))
         psum = ctx.enter_context(tc.psum_pool(name="psum", bufs=1))
 
         x_v_rows = consts.tile([P, P], BF16)
@@ -225,6 +227,21 @@ def tile_full_tmix_params_pb_v_kernel(
                     [P, PIECE, PACK], BF16, name="dv_grouped%d" % (k % 2), align_bytes=64
                 )
                 dv_grouped[k] = grouped
+            if k * M_TILES_PER_PIECE >= PAIRS_FROM:
+                for h in range(M_TILES_PER_PIECE):
+                    nc.vector.scalar_tensor_tensor(
+                        out=dv_grouped[k][:, h * M_TILE : (h + 1) * M_TILE, :],
+                        in0=columns_of(mix_loads, MIX_LOAD_ENDS, first, width).rearrange(
+                            "p j (i h) -> p h i j", h=M_TILES_PER_PIECE
+                        )[:, h, :, :],
+                        scalar=1.0,
+                        in1=columns_of(grad_loads, GRAD_LOAD_ENDS, first, width).rearrange(
+                            "p j (i h) -> p h i j", h=M_TILES_PER_PIECE
+                        )[:, h, :, :],
+                        op0=ALU.subtract,
+                        op1=ALU.mult,
+                    )
+                return
             nc.vector.scalar_tensor_tensor(
                 out=dv_grouped[k][:, first_col : first_col + width, :],
                 in0=columns_of(mix_loads, MIX_LOAD_ENDS, first, width).rearrange("p j w -> p w j"),
@@ -243,12 +260,19 @@ def tile_full_tmix_params_pb_v_kernel(
             )
 
         stages = {}
+        pairs = {}
 
         def multiply_and_store(m, first_chunk, chunks):
             rows = slice(m * M_TILE, (m + 1) * M_TILE)
             if m not in stages:
-                stage = stage_pool.tile([P, C], F32)
-                stages[m] = stage
+                if m >= PAIRS_FROM:
+                    both = pair_pool.tile([P, M_TILES_PER_PIECE, C], F32)
+                    for h in range(M_TILES_PER_PIECE):
+                        stages[m + h] = both[:, h, :]
+                    pairs[m] = both
+                else:
+                    single = stage_pool.tile([P, C], F32)
+                    stages[m] = single[:]
             stage = stages[m]
             for n in range(first_chunk, first_chunk + chunks):
                 cols = slice(n * CHUNK, (n + 1) * CHUNK)
@@ -269,7 +293,14 @@ def tile_full_tmix_params_pb_v_kernel(
                 else:
                     nc.scalar.copy(out=stage[:, cols], in_=product[:])
             cols = slice(first_chunk * CHUNK, (first_chunk + chunks) * CHUNK)
-            nc.sync.dma_start(out=out[rows, cols], in_=stage[:, cols])
+            if m < PAIRS_FROM:
+                nc.sync.dma_start(out=out[rows, cols], in_=stage[:, cols])
+            elif m % M_TILES_PER_PIECE == 1:
+                both_rows = slice((m - 1) * M_TILE, (m + 1) * M_TILE)
+                nc.sync.dma_start(
+                    out=out[both_rows, :].rearrange("(i h) c -> i h c", h=M_TILES_PER_PIECE),
+                    in_=pairs[m - 1][:],
+                )
 
         for s in range(STEPS + 2):
             if s < STEPS:

@@ -228,19 +228,19 @@ def tile_full_tmix_params_pb_v_kernel(
                 )
                 dv_grouped[k] = grouped
             if k * M_TILES_PER_PIECE >= PAIRS_FROM:
-                for h in range(M_TILES_PER_PIECE):
-                    nc.vector.scalar_tensor_tensor(
-                        out=dv_grouped[k][:, h * M_TILE : (h + 1) * M_TILE, :],
-                        in0=columns_of(mix_loads, MIX_LOAD_ENDS, first, width).rearrange(
-                            "p j (i h) -> p h i j", h=M_TILES_PER_PIECE
-                        )[:, h, :, :],
-                        scalar=1.0,
-                        in1=columns_of(grad_loads, GRAD_LOAD_ENDS, first, width).rearrange(
-                            "p j (i h) -> p h i j", h=M_TILES_PER_PIECE
-                        )[:, h, :, :],
-                        op0=ALU.subtract,
-                        op1=ALU.mult,
-                    )
+                h = first_col // M_TILE
+                nc.vector.scalar_tensor_tensor(
+                    out=dv_grouped[k][:, h * M_TILE : (h + 1) * M_TILE, :],
+                    in0=columns_of(mix_loads, MIX_LOAD_ENDS, k * PIECE, PIECE).rearrange(
+                        "p j (i h) -> p h i j", h=M_TILES_PER_PIECE
+                    )[:, h, :, :],
+                    scalar=1.0,
+                    in1=columns_of(grad_loads, GRAD_LOAD_ENDS, k * PIECE, PIECE).rearrange(
+                        "p j (i h) -> p h i j", h=M_TILES_PER_PIECE
+                    )[:, h, :, :],
+                    op0=ALU.subtract,
+                    op1=ALU.mult,
+                )
                 return
             nc.vector.scalar_tensor_tensor(
                 out=dv_grouped[k][:, first_col : first_col + width, :],
@@ -327,7 +327,7 @@ def tile_full_tmix_params_pb_v_kernel(
             if m >= EARLY_M_TILES:
                 multiply_and_store(m, 0, X_CHUNKS)
             k = m // M_TILES_PER_PIECE + 2
-            if k < DV_PIECES and m % M_TILES_PER_PIECE == 0:
-                dv_product(k, 0, PIECE)
-            if k < DV_PIECES and m % M_TILES_PER_PIECE == 1:
-                quantise_dv(k)
+            if m % M_TILES_PER_PIECE == 0 and 2 < k <= DV_PIECES:
+                quantise_dv(k - 1)
+            if k < DV_PIECES:
+                dv_product(k, m % M_TILES_PER_PIECE * M_TILE, M_TILE)

from contextlib import ExitStack

import concourse.mybir as mybir
from concourse.masks import make_identity

F32 = mybir.dt.float32
BF16 = mybir.dt.bfloat16
U32 = mybir.dt.uint32
U8 = mybir.dt.uint8
E4M3_X4 = mybir.dt.float8_e4m3fn_x4
E5M2_X4 = mybir.dt.float8_e5m2_x4
ALU = mybir.AluOpType

P = 128
PACK = 4
SEQS = 4
SEQ = 128
TOKENS = SEQS * SEQ
C = 2048
CO = 2048
CHUNK = 512
PIECE = CHUNK // 2
C_TILE = 128
C_TILES = C // C_TILE
PAIR = 2
STEP_COLS = PAIR * C_TILE
STEPS = C // STEP_COLS
STEPS_PER_CHUNK = CHUNK // STEP_COLS
M_TILE = 128
X_CHUNKS = C // CHUNK
M_TILES = CO // M_TILE
X_LOAD_ENDS = [CHUNK, 2 * CHUNK, C]
GRAD_LOAD_ENDS = [PIECE, CO]
MIX_LOAD_ENDS = [PIECE, 2 * CHUNK, CO]
LOAD_ORDER = ["x0", "x_v", "x1", "grad0", "mix0", "x2", "grad1", "mix1", "mix2"]
DV_PIECES = CO // PIECE
M_TILES_PER_PIECE = PIECE // M_TILE
BANKS = 8
STEP_BANKS = 4
WARM_UP_MATMULS = 4
FIRST_DV_STEP = 2
PAIRS_FROM = 8
EARLY_M_TILES = 2

FLOPS = 2 * TOKENS * CO * C
BYTES = 2 * TOKENS * C + 2 * C + 4 * TOKENS * CO + 2 * TOKENS * CO + 4 * CO * C


def tile_full_tmix_params_pb_v_kernel(
    tc, x, x_v, W_v, v_hid, v2, v0, v_first, mix, grad_out, out
):
    nc = tc.nc
    x_by_token = x.rearrange("b t c -> t b c")
    mix_rows = mix.rearrange("b (q j) c -> (b q) j c", j=PACK)
    grad_rows = grad_out.rearrange("b (q j) c -> (b q) j c", j=PACK)

    with ExitStack() as ctx:
        ctx.enter_context(tc.manual_schedule())
        consts = ctx.enter_context(tc.tile_pool(name="consts", bufs=1))
        inputs = ctx.enter_context(tc.tile_pool(name="inputs", bufs=1))
        keep = ctx.enter_context(tc.tile_pool(name="keep", bufs=1))
        work = ctx.enter_context(tc.tile_pool(name="work", bufs=3))
        stage_pool = ctx.enter_context(tc.tile_pool(name="stage", bufs=5))
        pair_pool = ctx.enter_context(tc.tile_pool(name="pair", bufs=3))
        psum = ctx.enter_context(tc.psum_pool(name="psum", bufs=1))

        x_v_rows = consts.tile([P, P], BF16)
        nc.vector.memset(x_v_rows[:], 0.0)

        def tiles_for(ends, dtype, name):
            tiles = []
            for i in range(len(ends)):
                width = ends[i] - ([0] + ends)[i]
                tiles.append(inputs.tile([P, PACK, width], dtype, name="%s%d" % (name, i)))
            return tiles

        x_loads = tiles_for(X_LOAD_ENDS, BF16, "x_load")
        grad_loads = tiles_for(GRAD_LOAD_ENDS, BF16, "grad_load")
        mix_loads = tiles_for(MIX_LOAD_ENDS, F32, "mix_load")

        def load(tiles, ends, i, rows):
            nc.sync.dma_start(out=tiles[i][:], in_=rows[:, :, ([0] + ends)[i] : ends[i]])

        def columns_of(tiles, ends, first_col, width):
            i = min([i for i in range(len(ends)) if first_col < ends[i]])
            first = first_col - ([0] + ends)[i]
            return tiles[i][:, :, first : first + width]

        for what in LOAD_ORDER:
            if what == "x_v":
                nc.sync.dma_start(
                    out=x_v_rows[0:C_TILES, :], in_=x_v.rearrange("a b (n c) -> (a b n) c", c=C_TILE)
                )
            elif what.startswith("x"):
                load(x_loads, X_LOAD_ENDS, int(what[1:]), x_by_token)
            elif what.startswith("grad"):
                load(grad_loads, GRAD_LOAD_ENDS, int(what[4:]), grad_rows)
            else:
                load(mix_loads, MIX_LOAD_ENDS, int(what[3:]), mix_rows)

        zeros = consts.tile([P, CHUNK], BF16)
        nc.vector.memset(zeros[:], 0.0)

        def idle_matmul(bank, width):
            nc.tensor.matmul(
                out=bank[:, 0:width], lhsT=zeros[:, 0:P], rhs=zeros[:, 0:width], start=True, stop=True
            )

        for i in range(WARM_UP_MATMULS):
            idle_bank = psum.tile([P, CHUNK], F32, tag="bank%d" % (1 + i % 2))
            idle_matmul(idle_bank, CHUNK)

        ident = consts.tile([P, P], BF16)
        make_identity(nc, ident[:])
        ident_words = consts.tile([P, P], F32)
        make_identity(nc, ident_words[:])
        shift_wide = consts.tile([P, P + 1], BF16)
        make_identity(nc, shift_wide[:, 1 : P + 1])
        nc.gpsimd.memset(shift_wide[:, 0:1], 0.0)
        minus_prev = consts.tile([P, P], BF16)
        nc.vector.tensor_tensor(
            out=minus_prev[:], in0=ident[:], in1=shift_wide[:, 0:P], op=ALU.subtract
        )

        def in_word_order(matrix, name):
            permuted = consts.tile([P, P], BF16, name=name)
            nc.vector.tensor_copy(
                out=permuted[:].rearrange("k (u q e) -> k u q e", u=2, e=2),
                in_=matrix.rearrange("k (q u e) -> k u q e", u=2, e=2),
            )
            return permuted

        ident_ordered = in_word_order(ident[:], "ident_ordered")
        minus_prev_ordered = in_word_order(minus_prev[:], "minus_prev_ordered")

        def tokens_of(turned, b):
            return turned.rearrange("c (u b j) -> c u b j", u=2, b=SEQS)[:, :, b, :]

        x_v_turned = psum.tile([P, P], BF16, tag="bank%d" % (BANKS - 1))
        nc.tensor.transpose(x_v_turned[:], x_v_rows[:], ident[:])
        x_v_cols = consts.tile([P, C_TILES], F32)
        nc.vector.tensor_copy(out=x_v_cols[:], in_=x_v_turned[:, 0:C_TILES])

        xv_codes = keep.tile([P, C], U32, align_bytes=64)
        xv_scales = keep.tile([P, C], U8, align_bytes=64)
        dv_codes = keep.tile([P, CO], U32, align_bytes=64)
        dv_scales = keep.tile([P, CO], U8, align_bytes=64)

        x_turned = {}
        xv_turned = {}
        xv_grouped = {}
        dv_grouped = {}

        def blocks_of(s):
            blocks = []
            for e in range(PAIR):
                x_tile = columns_of(x_loads, X_LOAD_ENDS, (s * PAIR + e) * C_TILE, C_TILE)
                for b in range(SEQS):
                    blocks.append((e, b, x_tile[:, b, :]))
            return blocks

        def turn_x(s):
            x_t = psum.tile([P, PAIR, TOKENS], BF16, tag="bank%d" % (s % 2 * STEP_BANKS))
            for e, b, block in blocks_of(s):
                nc.tensor.transpose(tokens_of(x_t[:, e, :], b), block, ident_ordered[:])
            x_t_sb = work.tile([P, PAIR, TOKENS], BF16)
            nc.scalar.copy(out=x_t_sb[:], in_=x_t[:])
            x_turned[s] = x_t_sb

        def xv_by_channel(s):
            bank = s % 2 * STEP_BANKS
            x_t_sb = x_turned[s]
            diff_t = []
            for e in range(PAIR):
                diff_t.append(
                    psum.tile([P, TOKENS], F32, tag="bank%d" % (bank + 1 + e), name="diff_t%d" % e)
                )
            for e, b, block in blocks_of(s):
                nc.tensor.matmul(
                    out=tokens_of(diff_t[e][:], b),
                    lhsT=block,
                    rhs=minus_prev_ordered[:],
                    start=True,
                    stop=True,
                )
            xv_t = work.tile([P, PAIR, TOKENS], BF16)
            for e in range(PAIR):
                n = s * PAIR + e
                nc.vector.scalar_tensor_tensor(
                    out=xv_t[:, e, :],
                    in0=diff_t[e][:],
                    scalar=x_v_cols[:, n : n + 1],
                    in1=x_t_sb[:, e, :],
                    op0=ALU.mult,
                    op1=ALU.subtract,
                )
            xv_turned[s] = xv_t

        def xv_by_token(s):
            bank = s % 2 * STEP_BANKS + STEP_BANKS - 1
            back = psum.tile([P, PAIR, 2, C_TILE], F32, tag="bank%d" % bank)
            for e in range(PAIR):
                words = xv_turned[s][:, e, :].bitcast(F32)
                for u in range(2):
                    nc.tensor.transpose(
                        back[:, e, u, :], words[:, u * P : (u + 1) * P], ident_words[:]
                    )
            grouped = work.tile([P, STEP_COLS * PACK], BF16, align_bytes=64)
            nc.scalar.copy(
                out=grouped[:].bitcast(F32).rearrange("p (e c u) -> p e c u", e=PAIR, u=2),
                in_=back[:].rearrange("p e u c -> p e c u"),
            )
            xv_grouped[s] = grouped

        def quantise_xv(s):
            cols = slice(s * STEP_COLS, (s + 1) * STEP_COLS)
            nc.vector.quantize_mx(
                out=xv_codes[:, cols].bitcast(E4M3_X4),
                scales=xv_scales[:, cols],
                in_=xv_grouped[s][:],
            )

        def dv_product(k, first_col, width):
            first = k * PIECE + first_col
            if k not in dv_grouped:
                grouped = work.tile(
                    [P, PIECE, PACK], BF16, name="dv_grouped%d" % (k % 2), align_bytes=64
                )
                dv_grouped[k] = grouped
            if k * M_TILES_PER_PIECE >= PAIRS_FROM:
                h = first_col // M_TILE
                nc.vector.scalar_tensor_tensor(
                    out=dv_grouped[k][:, h * M_TILE : (h + 1) * M_TILE, :],
                    in0=columns_of(mix_loads, MIX_LOAD_ENDS, k * PIECE, PIECE).rearrange(
                        "p j (i h) -> p h i j", h=M_TILES_PER_PIECE
                    )[:, h, :, :],
                    scalar=1.0,
                    in1=columns_of(grad_loads, GRAD_LOAD_ENDS, k * PIECE, PIECE).rearrange(
                        "p j (i h) -> p h i j", h=M_TILES_PER_PIECE
                    )[:, h, :, :],
                    op0=ALU.subtract,
                    op1=ALU.mult,
                )
                return
            nc.vector.scalar_tensor_tensor(
                out=dv_grouped[k][:, first_col : first_col + width, :],
                in0=columns_of(mix_loads, MIX_LOAD_ENDS, first, width).rearrange("p j w -> p w j"),
                scalar=1.0,
                in1=columns_of(grad_loads, GRAD_LOAD_ENDS, first, width).rearrange("p j w -> p w j"),
                op0=ALU.subtract,
                op1=ALU.mult,
            )

        def quantise_dv(k):
            cols = slice(k * PIECE, (k + 1) * PIECE)
            nc.vector.quantize_mx(
                out=dv_codes[:, cols].bitcast(E5M2_X4),
                scales=dv_scales[:, cols],
                in_=dv_grouped[k][:].rearrange("p w j -> p (w j)"),
            )

        stages = {}
        pairs = {}

        def multiply_and_store(m, first_chunk, chunks):
            rows = slice(m * M_TILE, (m + 1) * M_TILE)
            if m not in stages:
                if m >= PAIRS_FROM:
                    both = pair_pool.tile([P, M_TILES_PER_PIECE, C], F32)
                    for h in range(M_TILES_PER_PIECE):
                        stages[m + h] = both[:, h, :]
                    pairs[m] = both
                else:
                    single = stage_pool.tile([P, C], F32)
                    stages[m] = single[:]
            stage = stages[m]
            for n in range(first_chunk, first_chunk + chunks):
                cols = slice(n * CHUNK, (n + 1) * CHUNK)
                product = psum.tile(
                    [P, CHUNK], F32, tag="bank%d" % ((m * X_CHUNKS + n) % BANKS)
                )
                nc.tensor.matmul_mx(
                    out=product[:],
                    lhsT=dv_codes[:, rows].bitcast(E5M2_X4),
                    lhsT_scale=dv_scales[:, rows],
                    rhs=xv_codes[:, cols].bitcast(E4M3_X4),
                    rhs_scale=xv_scales[:, cols],
                    start=True,
                    stop=True,
                )
                if n % X_CHUNKS == 1:
                    nc.vector.tensor_copy(out=stage[:, cols], in_=product[:])
                else:
                    nc.scalar.copy(out=stage[:, cols], in_=product[:])
            cols = slice(first_chunk * CHUNK, (first_chunk + chunks) * CHUNK)
            if m < PAIRS_FROM:
                nc.sync.dma_start(out=out[rows, cols], in_=stage[:, cols])
            elif m % M_TILES_PER_PIECE == 1:
                both_rows = slice((m - 1) * M_TILE, (m + 1) * M_TILE)
                nc.sync.dma_start(
                    out=out[both_rows, :].rearrange("(i h) c -> i h c", h=M_TILES_PER_PIECE),
                    in_=pairs[m - 1][:],
                )

        for s in range(STEPS + 2):
            if s < STEPS:
                turn_x(s)
            if s >= 2:
                xv_by_token(s - 2)
            if s < STEPS:
                xv_by_channel(s)
            if s >= 2:
                quantise_xv(s - 2)
            if 0 <= s - FIRST_DV_STEP < M_TILES_PER_PIECE:
                dv_product(0, (s - FIRST_DV_STEP) * M_TILE, M_TILE)
            if s == FIRST_DV_STEP + M_TILES_PER_PIECE:
                quantise_dv(0)
            if s == STEPS + 1:
                quantise_dv(1)
            if s >= STEPS:
                multiply_and_store(s - STEPS, 0, X_CHUNKS - 1)
            if s == STEPS:
                dv_product(1, 0, PIECE)
        for m in range(EARLY_M_TILES):
            multiply_and_store(m, X_CHUNKS - 1, 1)
        for m in range(M_TILES):
            if m >= EARLY_M_TILES:
                multiply_and_store(m, 0, X_CHUNKS)
            k = m // M_TILES_PER_PIECE + 2
            if m % M_TILES_PER_PIECE == 0 and 2 < k <= DV_PIECES:
                quantise_dv(k - 1)
            if k < DV_PIECES:
                dv_product(k, m % M_TILES_PER_PIECE * M_TILE, M_TILE)
